import numpy as np
import ml_dtypes


def mxq(x, axis, fmt="e4m3"):
    dtype, down = {"e4m3": (ml_dtypes.float8_e4m3fn, 7), "e5m2": (ml_dtypes.float8_e5m2, 14)}[fmt]
    v = np.moveaxis(np.asarray(x, np.float32).astype(ml_dtypes.bfloat16).astype(np.float64), axis, -1)
    blocks = v.reshape(v.shape[:-1] + (-1, 32))
    amax = np.abs(blocks).max(-1, keepdims=True)
    byte = np.maximum(np.where(amax > 0, np.frexp(amax)[1] - 1 + 127, 0) - down, 1)
    scale = np.exp2(byte - 127.0)
    codes = (blocks / scale).astype(np.float32).astype(dtype).astype(np.float64)
    return np.moveaxis((codes * scale).reshape(v.shape), -1, axis)


WIDE = False


def mx_kscale(k):
    if not WIDE:
        return np.ones(k)
    levels = np.array([10, -10, 5, -5, 0])
    a = np.random.permutation(np.resize(levels, k // 512 * 4)).reshape(k // 512, 4)
    idx = np.arange(k)
    return np.exp2(a[idx // 512, idx % 128 // 32])


BF16 = ml_dtypes.bfloat16


def bf(x):
    return np.asarray(x, np.float32).astype(BF16)


def f64(x):
    return np.asarray(x).astype(np.float64)


B, D_IN, D_HID, SHARE = 4096, 1024, 128, 2
NUM_GATE = 4 + SHARE


def sigmoid(v):
    return 1.0 / (1.0 + np.exp(-v))


def setup_inputs():
    s = mx_kscale(D_IN)
    n = np.random.standard_normal
    return {
        "input": bf(n((B, D_IN)) * s),
        "h_minors": bf(n((B, D_HID))),
        "c_minors": bf(n((B, D_HID))),
        "s_minors": bf(n((SHARE, B, D_HID))),
        "mask": bf(np.random.uniform(0.5, 1.5, B)),
        "weight_ih": bf(n((NUM_GATE * D_HID, D_IN)) * 0.7 / np.sqrt(D_IN) / s),
        "weight_hh": bf(n((4 * D_HID, D_HID)) * 0.7 / np.sqrt(D_HID)),
        "weight_sh": bf(n((SHARE * D_HID, D_HID)) * 0.7 / np.sqrt(D_HID)),
        "bias_ih": bf(n(NUM_GATE * D_HID) * 0.3),
        "bias_hh": bf(n(4 * D_HID) * 0.3),
        "bias_sh": bf(n(SHARE * D_HID) * 0.3),
        "idx": 0,
    }


def reference(input, h_minors, c_minors, s_minors, mask, weight_ih, weight_hh, weight_sh, bias_ih, bias_hh, bias_sh, idx):
    H = weight_hh.shape[1]
    share = weight_sh.shape[0] // H
    m = f64(mask)[:, None]
    tmp = (mxq(f64(input), 1, "e4m3") @ mxq(f64(weight_ih), 1, "e4m3").T) + f64(bias_ih)
    tmp2 = f64(h_minors) @ f64(weight_hh).T + f64(bias_hh)
    tmp3 = f64(s_minors)[idx] @ f64(weight_sh).T + f64(bias_sh)
    tmp_in, tmp_s = tmp[:, :4 * H], tmp[:, 4 * H:]
    z = tmp_in + tmp2
    ifo = sigmoid(z[:, :3 * H])
    i, f, o = ifo[:, :H], ifo[:, H:2 * H], ifo[:, 2 * H:]
    c_hat = z[:, 3 * H:]
    b = sigmoid(tmp_s + tmp3)
    c_t = (f * f64(c_minors) + i * np.tanh(c_hat)) * m
    tc = np.tanh(c_t) * m
    h = o * tc
    s = b.reshape(-1, share, H) * tc[:, None, :]
    s = np.moveaxis(s, 1, 0)
    return (h, c_t, s[0], s[1])

@@ -1,0 +1,340 @@
+from contextlib import ExitStack
+
+import concourse.mybir as mybir
+from concourse.masks import make_identity
+
+F32 = mybir.dt.float32
+BF16 = mybir.dt.bfloat16
+U32 = mybir.dt.uint32
+U8 = mybir.dt.uint8
+FP8X4 = mybir.dt.float8_e4m3fn_x4
+ACT = mybir.ActivationFunctionType
+ALU = mybir.AluOpType
+
+P = 128
+B = 4096
+D_IN = 1024
+H = 128
+NG = 768
+NT = B // P
+NPAIR = NT // 2
+NGROUP = NT // 4
+LA = 2
+PINNED = False
+V_GROUPS = 1
+
+FLOPS = 2 * B * (D_IN * NG + H * 512 + H * 256)
+BYTES = 2 * (B * D_IN + 3 * B * H + B + NG * D_IN + 768 * H + 2 * NG) + 4 * 4 * B * H
+
+
+def tile_share_lstm_cell_t_kernel(
+    tc, x_in, h_minors, c_minors, s_minors, mask, weight_ih, weight_hh, weight_sh,
+    bias_ih, bias_hh, bias_sh, idx, out_0, out_1, out_2, out_3,
+):
+    nc = tc.nc
+    with ExitStack() as ctx:
+        const = ctx.enter_context(tc.tile_pool(name="const", bufs=1))
+        xpool = ctx.enter_context(tc.tile_pool(name="xpool", bufs=4))
+        qpool = ctx.enter_context(tc.tile_pool(name="qpool", bufs=3))
+        pbpool = ctx.enter_context(tc.tile_pool(name="pbpool", bufs=LA + 1))
+        gpool = ctx.enter_context(tc.tile_pool(name="gpool", bufs=5))
+        opool = ctx.enter_context(tc.tile_pool(name="opool", bufs=2))
+        psum = ctx.enter_context(tc.psum_pool(name="psum", bufs=1))
+        if PINNED:
+            ctx.enter_context(tc.manual_schedule())
+
+        xv = x_in.rearrange("(p t) k -> p t k", t=NT)
+        hv = h_minors.rearrange("(p t) k -> p t k", t=NT)
+        cv = c_minors.rearrange("(p t) k -> p t k", t=NT)
+        sv = s_minors[idx].rearrange("(p t) k -> p t k", t=NT)
+        outs = [o.rearrange("(p t) k -> p t k", t=NT) for o in (out_0, out_1, out_2, out_3)]
+
+        whh_raw = const.tile([P, 6, H], BF16)
+        braw = const.tile([P, NG], BF16)
+        m_bf = const.tile([P, NT], BF16)
+        w_raw = const.tile([P, 6, D_IN], BF16)
+        h_sb = const.tile([P, NT, H], BF16)
+        s_sb = const.tile([P, NT, H], BF16)
+        c_sb = const.tile([P, NT, H], BF16)
+        nc.vector.memset(braw[:], 0.0)
+        nc.scalar.dma_start(out=whh_raw[:, 0:4, :], in_=weight_hh.rearrange("(j p) k -> p j k", p=P))
+        nc.scalar.dma_start(out=whh_raw[:, 4:6, :], in_=weight_sh.rearrange("(j p) k -> p j k", p=P))
+        nc.scalar.dma_start(out=braw[0:1, :], in_=bias_ih.unsqueeze(0))
+        nc.scalar.dma_start(out=braw[1:2, 0:512], in_=bias_hh.unsqueeze(0))
+        nc.scalar.dma_start(out=braw[1:2, 512:768], in_=bias_sh.unsqueeze(0))
+        nc.scalar.dma_start(out=m_bf[:], in_=mask.rearrange("(p t) -> p t", t=NT))
+        nc.sync.dma_start(out=h_sb[:, 0:8, :], in_=hv[:, 0:8, :])
+        nc.sync.dma_start(out=s_sb[:, 0:8, :], in_=sv[:, 0:8, :])
+        nc.sync.dma_start(out=w_raw[:], in_=weight_ih.rearrange("(j p) k -> p j k", p=P))
+        x_tiles = []
+
+        def load_x(ch):
+            x_sb = xpool.tile([P, 4, D_IN], BF16, name="x_sb")
+            nc.sync.dma_start(out=x_sb[:], in_=xv[:, 4 * ch:4 * ch + 4, :])
+            x_tiles.append(x_sb)
+
+        load_x(0)
+        nc.sync.dma_start(out=h_sb[:, 8:NT, :], in_=hv[:, 8:NT, :])
+        nc.sync.dma_start(out=s_sb[:, 8:NT, :], in_=sv[:, 8:NT, :])
+        load_x(1)
+        nc.sync.dma_start(out=c_sb[:], in_=cv)
+        load_x(2)
+        load_x(3)
+
+        ident_f = const.tile([P, P], F32)
+        ident_b = const.tile([P, P], BF16)
+        ones = const.tile([P, P], BF16)
+        make_identity(nc, ident_b[:])
+        make_identity(nc, ident_f[:])
+        nc.vector.memset(ones[:], 1.0)
+        m32 = const.tile([P, NT], F32)
+        nc.vector.tensor_copy(out=m32[:], in_=m_bf[:])
+
+        wT = const.tile([P, NG], BF16)
+        wt_ps = psum.tile([P, 6, H], BF16, tag="X0", name="wt_ps")
+        for j in range(6):
+            nc.tensor.transpose(wt_ps[:, j, :], whh_raw[:, j, :], ident_b[:])
+        nc.vector.tensor_copy(out=wT[:], in_=wt_ps[:].rearrange("p j k -> p (j k)"))
+
+        bias_bc = const.tile([P, NG], F32)
+        b_ps0 = psum.tile([P, 512], F32, tag="P0", name="b_ps0")
+        b_ps1 = psum.tile([P, 512], F32, tag="PC", name="b_ps1")
+        nc.tensor.matmul(out=b_ps0[:], lhsT=ones[:], rhs=braw[:, 0:512], start=True, stop=True)
+        nc.tensor.matmul(out=b_ps1[:, 0:256], lhsT=ones[:], rhs=braw[:, 512:768], start=True, stop=True)
+        nc.vector.tensor_copy(out=bias_bc[:, 0:512], in_=b_ps0[:])
+        nc.vector.tensor_copy(out=bias_bc[:, 512:768], in_=b_ps1[:, 0:256])
+
+        hsT = const.tile([P, NGROUP, 2, 4, H], BF16)
+
+        def hs_transposes(gi, eng):
+            hs_ps = psum.tile([P, 2, 4, H], BF16, tag="X%d" % (gi % 2), name="hs_ps")
+            for tt in range(4):
+                nc.tensor.transpose(hs_ps[:, 0, tt, :], h_sb[:, 4 * gi + tt, :], ident_b[:])
+            for tt in range(4):
+                nc.tensor.transpose(hs_ps[:, 1, tt, :], s_sb[:, 4 * gi + tt, :], ident_b[:])
+            if eng == 0:
+                nc.vector.tensor_copy(out=hsT[:, gi], in_=hs_ps[:])
+            else:
+                nc.scalar.copy(out=hsT[:, gi], in_=hs_ps[:])
+
+        hs_transposes(0, 0)
+        hs_transposes(1, 1)
+
+        w_grp = const.tile([P, 2, NG, 2], F32, align_bytes=64)
+        w_codes = const.tile([P, 2 * NG], U32, align_bytes=64)
+        w_scales = const.tile([P, 2 * NG], U8, align_bytes=64)
+        for j in range(6):
+            w_ps = psum.tile([P, 4, P], F32, tag=("A0", "A1", "AC")[j % 3], name="w_ps")
+            ww = w_raw[:, j, :].bitcast(F32)
+            for q in range(4):
+                nc.tensor.transpose(w_ps[:, q, :], ww[:, P * q:P * q + P], ident_f[:])
+            src = w_ps[:].rearrange("p (g u) r -> p g r u", g=2)
+            if j % 2 == 0:
+                nc.scalar.copy(out=w_grp[:, :, P * j:P * j + P, :], in_=src)
+            else:
+                nc.vector.tensor_copy(out=w_grp[:, :, P * j:P * j + P, :], in_=src)
+        wg_bf = w_grp[:].rearrange("p g n u -> p (g n u)").bitcast(BF16)
+        nc.vector.quantize_mx(out=w_codes[:, 0:1024].bitcast(FP8X4), scales=w_scales[:, 0:1024], in_=wg_bf[:, 0:4096])
+        nc.vector.quantize_mx(out=w_codes[:, 1024:1536].bitcast(FP8X4), scales=w_scales[:, 1024:1536], in_=wg_bf[:, 4096:6144])
+
+        xg_t = {}
+        xq_t = {}
+        pl_t = {}
+        pb_t = {}
+        mx_t = {}
+        g4_t = {}
+        out_t = {}
+
+        def x_transposes(k):
+            xg = qpool.tile([P, 2, 2, P, 2], F32, align_bytes=64, name="xg")
+            xg_t[k] = xg
+            for i in range(2):
+                t = 2 * k + i
+                xt = psum.tile([P, 4, P], F32, tag="X%d" % i, name="xt")
+                xw = x_tiles[t // 4][:, t % 4, :].bitcast(F32)
+                for q in range(4):
+                    nc.tensor.transpose(xt[:, q, :], xw[:, P * q:P * q + P], ident_f[:])
+                nc.scalar.copy(out=xg[:, i], in_=xt[:].rearrange("p (g u) r -> p g r u", g=2))
+
+        def quantise(k):
+            xc = qpool.tile([P, 512], U32, align_bytes=64, name="xc")
+            xs = qpool.tile([P, 512], U8, align_bytes=64, name="xs")
+            xq_t[k] = (xc, xs)
+            nc.vector.quantize_mx(
+                out=xc[:].bitcast(FP8X4), scales=xs[:],
+                in_=xg_t[k][:].rearrange("p t g r u -> p (t g r u)").bitcast(BF16),
+            )
+
+        def plain(k):
+            gi = k // 2
+            tt = 2 * (k % 2)
+            p0 = psum.tile([P, 512], F32, tag="P0", name="p0")
+            p1 = psum.tile([P, 512], F32, tag="P1", name="p1")
+            pc = psum.tile([P, 512], F32, tag="PC", name="pc")
+            pl_t[k] = (p0, p1, pc)
+            nc.tensor.matmul(out=p0[:], lhsT=hsT[:, gi, 0, tt, :], rhs=wT[:, 0:512], start=True, stop=True)
+            nc.tensor.matmul(out=p1[:], lhsT=hsT[:, gi, 0, tt + 1, :], rhs=wT[:, 0:512], start=True, stop=True)
+            nc.tensor.matmul(out=pc[:, 0:256], lhsT=hsT[:, gi, 1, tt, :], rhs=wT[:, 512:768], start=True, stop=True)
+            nc.tensor.matmul(out=pc[:, 256:512], lhsT=hsT[:, gi, 1, tt + 1, :], rhs=wT[:, 512:768], start=True, stop=True)
+
+        def add_bias(k):
+            p0, p1, pc = pl_t[k]
+            pb = pbpool.tile([P, 2, NG], F32, name="pb")
+            pb_t[k] = pb
+            nc.vector.tensor_tensor(out=pb[:, 0, 0:512], in0=p0[:], in1=bias_bc[:, 0:512], op=ALU.add)
+            nc.vector.tensor_tensor(out=pb[:, 1, 0:512], in0=p1[:], in1=bias_bc[:, 0:512], op=ALU.add)
+            nc.vector.tensor_tensor(
+                out=pb[:, :, 512:768], in0=pc[:].rearrange("p (t n) -> p t n", t=2),
+                in1=bias_bc[:, 512:768].unsqueeze(1).to_broadcast([P, 2, 256]), op=ALU.add,
+            )
+
+        def mx(k):
+            xc, xs = xq_t[k]
+            a0 = psum.tile([P, 512], F32, tag="A0", name="a0")
+            a1 = psum.tile([P, 512], F32, tag="A1", name="a1")
+            ac = psum.tile([P, 512], F32, tag="AC", name="ac")
+            mx_t[k] = (a0, a1, ac)
+            for i in range(2):
+                dst = (a0, a1)[i]
+                for g in range(2):
+                    lo = (2 * i + g) * P
+                    nc.tensor.matmul_mx(
+                        out=dst[:], lhsT=xc[:, lo:lo + P].bitcast(FP8X4), lhsT_scale=xs[:, lo:lo + P],
+                        rhs=w_codes[:, g * NG:g * NG + 512].bitcast(FP8X4), rhs_scale=w_scales[:, g * NG:g * NG + 512],
+                        start=(g == 0), stop=(g == 1),
+                    )
+            for i in range(2):
+                for g in range(2):
+                    lo = (2 * i + g) * P
+                    nc.tensor.matmul_mx(
+                        out=ac[:, 256 * i:256 * i + 256], lhsT=xc[:, lo:lo + P].bitcast(FP8X4), lhsT_scale=xs[:, lo:lo + P],
+                        rhs=w_codes[:, g * NG + 512:g * NG + 768].bitcast(FP8X4), rhs_scale=w_scales[:, g * NG + 512:g * NG + 768],
+                        start=(g == 0), stop=(g == 1),
+                    )
+
+        def add_mx(k):
+            gi = k // 2
+            tt = 2 * (k % 2)
+            if tt == 0:
+                g4_new = gpool.tile([P, 4, NG], F32, name="g4")
+                g4_t[gi] = g4_new
+            g4 = g4_t[gi]
+            a0, a1, ac = mx_t[k]
+            pb = pb_t[k]
+            nc.vector.tensor_tensor(out=g4[:, tt, 0:512], in0=a0[:], in1=pb[:, 0, 0:512], op=ALU.add)
+            nc.vector.tensor_tensor(out=g4[:, tt + 1, 0:512], in0=a1[:], in1=pb[:, 1, 0:512], op=ALU.add)
+            nc.vector.tensor_tensor(
+                out=g4[:, tt:tt + 2, 512:768], in0=ac[:].rearrange("p (t n) -> p t n", t=2),
+                in1=pb[:, :, 512:768], op=ALU.add,
+            )
+
+        def gate_functions(k):
+            g4 = g4_t[k // 2]
+            tt = 2 * (k % 2)
+            nc.scalar.activation(out=g4[:, tt:tt + 2, 0:384], in_=g4[:, tt:tt + 2, 0:384], func=ACT.Sigmoid)
+            nc.scalar.activation(out=g4[:, tt:tt + 2, 384:512], in_=g4[:, tt:tt + 2, 384:512], func=ACT.Tanh)
+            nc.scalar.activation(out=g4[:, tt:tt + 2, 512:768], in_=g4[:, tt:tt + 2, 512:768], func=ACT.Sigmoid)
+
+        def out_tiles(gi):
+            oh = opool.tile([P, 4, H], F32, name="oh")
+            oc = opool.tile([P, 4, H], F32, name="oc")
+            os_ = opool.tile([P, 2, 4, H], F32, name="os_")
+            out_t[gi] = (oh, oc, os_)
+
+        def cell_sum_gpsimd(gi):
+            g4 = g4_t[gi]
+            nc.gpsimd.tensor_tensor(out=g4[:, :, 128:256], in0=g4[:, :, 128:256], in1=c_sb[:, 4 * gi:4 * gi + 4, :], op=ALU.mult)
+            nc.gpsimd.tensor_tensor(out=g4[:, :, 384:512], in0=g4[:, :, 0:128], in1=g4[:, :, 384:512], op=ALU.mult)
+            nc.gpsimd.tensor_tensor(out=g4[:, :, 0:128], in0=g4[:, :, 128:256], in1=g4[:, :, 384:512], op=ALU.add)
+
+        def cell_scalar(gi, tt):
+            g4 = g4_t[gi]
+            oc = out_t[gi][1]
+            m = m32[:, 4 * gi + tt:4 * gi + tt + 1]
+            nc.scalar.activation(out=g4[:, tt, 128:256], in_=g4[:, tt, 0:128], func=ACT.Tanh, scale=m)
+            nc.scalar.activation(out=oc[:, tt, :], in_=g4[:, tt, 0:128], func=ACT.Copy, scale=m)
+            nc.scalar.activation(out=g4[:, tt, 384:512], in_=g4[:, tt, 128:256], func=ACT.Copy, scale=m)
+
+        def outputs_gpsimd(gi):
+            g4 = g4_t[gi]
+            oh, oc, os_ = out_t[gi]
+            nc.gpsimd.tensor_tensor(out=oh[:], in0=g4[:, :, 256:384], in1=g4[:, :, 384:512], op=ALU.mult)
+            nc.gpsimd.tensor_tensor(
+                out=os_[:].rearrange("p k t c -> p t k c"),
+                in0=g4[:, :, 512:768].rearrange("p t (k c) -> p t k c", k=2),
+                in1=g4[:, :, 384:512].unsqueeze(2).to_broadcast([P, 4, 2, H]), op=ALU.mult,
+            )
+
+        def cell_vector(gi, tt):
+            g4 = g4_t[gi]
+            oh, oc, os_ = out_t[gi]
+            t = 4 * gi + tt
+            m = m32[:, t:t + 1]
+            nc.vector.scalar_tensor_tensor(out=g4[:, tt, 128:256], in0=c_sb[:, t, :], scalar=m, in1=g4[:, tt, 128:256], op0=ALU.mult, op1=ALU.mult)
+            nc.vector.scalar_tensor_tensor(out=g4[:, tt, 384:512], in0=g4[:, tt, 384:512], scalar=m, in1=g4[:, tt, 0:128], op0=ALU.mult, op1=ALU.mult)
+            nc.vector.tensor_tensor(out=oc[:, tt, :], in0=g4[:, tt, 128:256], in1=g4[:, tt, 384:512], op=ALU.add)
+            nc.scalar.activation(out=g4[:, tt, 0:128], in_=oc[:, tt, :], func=ACT.Tanh)
+
+        def outputs_vector(gi, tt):
+            g4 = g4_t[gi]
+            oh, oc, os_ = out_t[gi]
+            m = m32[:, 4 * gi + tt:4 * gi + tt + 1]
+            nc.vector.scalar_tensor_tensor(out=oh[:, tt, :], in0=g4[:, tt, 0:128], scalar=m, in1=g4[:, tt, 256:384], op0=ALU.mult, op1=ALU.mult)
+            nc.vector.scalar_tensor_tensor(
+                out=os_[:, :, tt, :], in0=g4[:, tt, 0:128].unsqueeze(1).to_broadcast([P, 2, H]), scalar=m,
+                in1=g4[:, tt, 512:768].rearrange("p (k c) -> p k c", k=2), op0=ALU.mult, op1=ALU.mult,
+            )
+
+        def store(gi, which):
+            oh, oc, os_ = out_t[gi]
+            src = (oh[:], oc[:], os_[:, 0], os_[:, 1])[which]
+            nc.sync.dma_start(out=outs[which][:, 4 * gi:4 * gi + 4, :], in_=src)
+
+        NGP = NGROUP - V_GROUPS
+        for j in range(-3, NPAIR + 8):
+            if 0 <= j + 1 < NPAIR:
+                mx(j + 1)
+            if 0 <= j + 3 < NPAIR:
+                if (j + 3) % 2 == 0 and (j + 3) // 2 + 2 < NGROUP and (j + 3) // 2 + 2 >= 4:
+                    load_x((j + 3) // 2 + 2)
+                x_transposes(j + 3)
+            kk = j + 2 + LA
+            if kk % 2 == 0 and 2 <= kk // 2 < NGROUP:
+                hs_transposes(kk // 2, 1)
+            if 0 <= j + 1 + LA < NPAIR:
+                plain(j + 1 + LA)
+            if 0 <= j < NPAIR:
+                add_mx(j)
+            if 0 <= j + 2 < NPAIR:
+                quantise(j + 2)
+            if 0 <= j + LA < NPAIR:
+                add_bias(j + LA)
+            if 0 <= j - 1 < NPAIR:
+                gate_functions(j - 1)
+            if (j - 3) % 2 == 0 and 0 <= (j - 3) // 2 < NGP:
+                out_tiles((j - 3) // 2)
+                cell_sum_gpsimd((j - 3) // 2)
+            if (j - 4) % 2 == 0 and 0 <= (j - 4) // 2 < NGP:
+                cell_scalar((j - 4) // 2, 0)
+                cell_scalar((j - 4) // 2, 1)
+            if (j - 5) % 2 == 0 and 0 <= (j - 5) // 2 < NGP:
+                cell_scalar((j - 5) // 2, 2)
+                cell_scalar((j - 5) // 2, 3)
+                store((j - 5) // 2, 1)
+            if (j - 6) % 2 == 0 and 0 <= (j - 6) // 2 < NGP:
+                outputs_gpsimd((j - 6) // 2)
+                store((j - 6) // 2, 0)
+                store((j - 6) // 2, 2)
+                store((j - 6) // 2, 3)
+            if 0 <= j - 2 < NPAIR and (j - 2) // 2 >= NGP:
+                gi = (j - 2) // 2
+                tt = 2 * ((j - 2) % 2)
+                if tt == 0:
+                    out_tiles(gi)
+                cell_vector(gi, tt)
+                cell_vector(gi, tt + 1)
+                outputs_vector(gi, tt)
+                outputs_vector(gi, tt + 1)
+                if tt == 2:
+                    for which in (1, 0, 2, 3):
+                        store(gi, which)

@@ -19,8 +19,10 @@ NG = 768
 NT = B // P
 NPAIR = NT // 2
 NGROUP = NT // 4
-LA = 2
-PINNED = False
+LA = 1
+XL = 3
+QL = 2
+PINNED = True
 V_GROUPS = 1
 
 FLOPS = 2 * B * (D_IN * NG + H * 512 + H * 256)
@@ -34,11 +36,11 @@ def tile_share_lstm_cell_t_kernel(
     nc = tc.nc
     with ExitStack() as ctx:
         const = ctx.enter_context(tc.tile_pool(name="const", bufs=1))
-        xpool = ctx.enter_context(tc.tile_pool(name="xpool", bufs=4))
+        xpool = ctx.enter_context(tc.tile_pool(name="xpool", bufs=8))
         qpool = ctx.enter_context(tc.tile_pool(name="qpool", bufs=3))
         pbpool = ctx.enter_context(tc.tile_pool(name="pbpool", bufs=LA + 1))
         gpool = ctx.enter_context(tc.tile_pool(name="gpool", bufs=5))
-        opool = ctx.enter_context(tc.tile_pool(name="opool", bufs=2))
+        opool = ctx.enter_context(tc.tile_pool(name="opool", bufs=3))
         psum = ctx.enter_context(tc.psum_pool(name="psum", bufs=1))
         if PINNED:
             ctx.enter_context(tc.manual_schedule())
@@ -47,114 +49,113 @@ def tile_share_lstm_cell_t_kernel(
         hv = h_minors.rearrange("(p t) k -> p t k", t=NT)
         cv = c_minors.rearrange("(p t) k -> p t k", t=NT)
         sv = s_minors[idx].rearrange("(p t) k -> p t k", t=NT)
+        wv = weight_ih.rearrange("(j p) k -> p j k", p=P)
         outs = [o.rearrange("(p t) k -> p t k", t=NT) for o in (out_0, out_1, out_2, out_3)]
 
         whh_raw = const.tile([P, 6, H], BF16)
         braw = const.tile([P, NG], BF16)
         m_bf = const.tile([P, NT], BF16)
+        m32 = const.tile([P, NT], F32)
         w_raw = const.tile([P, 6, D_IN], BF16)
         h_sb = const.tile([P, NT, H], BF16)
         s_sb = const.tile([P, NT, H], BF16)
         c_sb = const.tile([P, NT, H], BF16)
-        nc.vector.memset(braw[:], 0.0)
-        nc.scalar.dma_start(out=whh_raw[:, 0:4, :], in_=weight_hh.rearrange("(j p) k -> p j k", p=P))
-        nc.scalar.dma_start(out=whh_raw[:, 4:6, :], in_=weight_sh.rearrange("(j p) k -> p j k", p=P))
-        nc.scalar.dma_start(out=braw[0:1, :], in_=bias_ih.unsqueeze(0))
-        nc.scalar.dma_start(out=braw[1:2, 0:512], in_=bias_hh.unsqueeze(0))
-        nc.scalar.dma_start(out=braw[1:2, 512:768], in_=bias_sh.unsqueeze(0))
-        nc.scalar.dma_start(out=m_bf[:], in_=mask.rearrange("(p t) -> p t", t=NT))
-        nc.sync.dma_start(out=h_sb[:, 0:8, :], in_=hv[:, 0:8, :])
-        nc.sync.dma_start(out=s_sb[:, 0:8, :], in_=sv[:, 0:8, :])
-        nc.sync.dma_start(out=w_raw[:], in_=weight_ih.rearrange("(j p) k -> p j k", p=P))
-        x_tiles = []
-
-        def load_x(ch):
-            x_sb = xpool.tile([P, 4, D_IN], BF16, name="x_sb")
-            nc.sync.dma_start(out=x_sb[:], in_=xv[:, 4 * ch:4 * ch + 4, :])
-            x_tiles.append(x_sb)
-
-        load_x(0)
-        nc.sync.dma_start(out=h_sb[:, 8:NT, :], in_=hv[:, 8:NT, :])
-        nc.sync.dma_start(out=s_sb[:, 8:NT, :], in_=sv[:, 8:NT, :])
-        load_x(1)
-        nc.sync.dma_start(out=c_sb[:], in_=cv)
-        load_x(2)
-        load_x(3)
-
         ident_f = const.tile([P, P], F32)
         ident_b = const.tile([P, P], BF16)
         ones = const.tile([P, P], BF16)
+        wT = const.tile([P, NG], BF16)
+        bias_bc = const.tile([P, NG], F32)
+        hsT = const.tile([P, NGROUP, 2, 4, H], BF16)
+        w_grp = const.tile([P, 2, NG, 2], F32, align_bytes=64)
+        w_codes = const.tile([P, 2 * NG], U32, align_bytes=64)
+        w_scales = const.tile([P, 2 * NG], U8, align_bytes=64)
+
+        xp_t = {}
+        ps_t = {}
+        xg_t = {}
+        xq_t = {}
+        pb_t = {}
+        g4_t = {}
+        out_t = {}
+
+        def load_x(k):
+            x_sb = xpool.tile([P, 2, D_IN], BF16, name="x_sb")
+            nc.sync.dma_start(out=x_sb[:], in_=xv[:, 2 * k:2 * k + 2, :])
+            xp_t[k] = x_sb
+
+        def copy_out(eng, out, in_):
+            if eng == "V":
+                nc.vector.tensor_copy(out=out, in_=in_)
+            else:
+                nc.scalar.copy(out=out, in_=in_)
+
+        nc.vector.memset(braw[:], 0.0)
+        nc.vector.memset(ones[:], 1.0)
         make_identity(nc, ident_b[:])
         make_identity(nc, ident_f[:])
-        nc.vector.memset(ones[:], 1.0)
-        m32 = const.tile([P, NT], F32)
-        nc.vector.tensor_copy(out=m32[:], in_=m_bf[:])
+        nc.scalar.dma_start(out=braw[0:1, :], in_=bias_ih.unsqueeze(0))
+        nc.scalar.dma_start(out=braw[1:2, 0:512], in_=bias_hh.unsqueeze(0))
+        nc.scalar.dma_start(out=braw[1:2, 512:768], in_=bias_sh.unsqueeze(0))
+        nc.sync.dma_start(out=whh_raw[:, 0:4, :], in_=weight_hh.rearrange("(j p) k -> p j k", p=P))
+        nc.sync.dma_start(out=whh_raw[:, 4:6, :], in_=weight_sh.rearrange("(j p) k -> p j k", p=P))
+        nc.sync.dma_start(out=h_sb[:, 0:8, :], in_=hv[:, 0:8, :])
+        nc.sync.dma_start(out=s_sb[:, 0:8, :], in_=sv[:, 0:8, :])
+        nc.sync.dma_start(out=w_raw[:, 0:2, :], in_=wv[:, 0:2, :])
+        nc.sync.dma_start(out=w_raw[:, 2:4, :], in_=wv[:, 2:4, :])
+        load_x(0)
+        nc.sync.dma_start(out=w_raw[:, 4:6, :], in_=wv[:, 4:6, :])
+        load_x(1)
+        nc.scalar.dma_start(out=m_bf[:], in_=mask.rearrange("(p t) -> p t", t=NT))
+        load_x(2)
+        nc.sync.dma_start(out=h_sb[:, 8:NT, :], in_=hv[:, 8:NT, :])
+        nc.sync.dma_start(out=s_sb[:, 8:NT, :], in_=sv[:, 8:NT, :])
+        load_x(3)
+        nc.sync.dma_start(out=c_sb[:], in_=cv)
+        for k in range(4, 8):
+            load_x(k)
 
-        wT = const.tile([P, NG], BF16)
-        wt_ps = psum.tile([P, 6, H], BF16, tag="X0", name="wt_ps")
-        for j in range(6):
-            nc.tensor.transpose(wt_ps[:, j, :], whh_raw[:, j, :], ident_b[:])
-        nc.vector.tensor_copy(out=wT[:], in_=wt_ps[:].rearrange("p j k -> p (j k)"))
-
-        bias_bc = const.tile([P, NG], F32)
-        b_ps0 = psum.tile([P, 512], F32, tag="P0", name="b_ps0")
-        b_ps1 = psum.tile([P, 512], F32, tag="PC", name="b_ps1")
-        nc.tensor.matmul(out=b_ps0[:], lhsT=ones[:], rhs=braw[:, 0:512], start=True, stop=True)
-        nc.tensor.matmul(out=b_ps1[:, 0:256], lhsT=ones[:], rhs=braw[:, 512:768], start=True, stop=True)
-        nc.vector.tensor_copy(out=bias_bc[:, 0:512], in_=b_ps0[:])
-        nc.vector.tensor_copy(out=bias_bc[:, 512:768], in_=b_ps1[:, 0:256])
-
-        hsT = const.tile([P, NGROUP, 2, 4, H], BF16)
-
-        def hs_transposes(gi, eng):
-            hs_ps = psum.tile([P, 2, 4, H], BF16, tag="X%d" % (gi % 2), name="hs_ps")
+        def hs_pe(gi, tag):
+            hs_ps = psum.tile([P, 2, 4, H], BF16, tag=tag, name="hs_ps")
+            ps_t["hs", gi] = hs_ps
             for tt in range(4):
                 nc.tensor.transpose(hs_ps[:, 0, tt, :], h_sb[:, 4 * gi + tt, :], ident_b[:])
             for tt in range(4):
                 nc.tensor.transpose(hs_ps[:, 1, tt, :], s_sb[:, 4 * gi + tt, :], ident_b[:])
-            if eng == 0:
-                nc.vector.tensor_copy(out=hsT[:, gi], in_=hs_ps[:])
-            else:
-                nc.scalar.copy(out=hsT[:, gi], in_=hs_ps[:])
 
-        hs_transposes(0, 0)
-        hs_transposes(1, 1)
+        def hs_ev(gi, eng):
+            copy_out(eng, hsT[:, gi], ps_t["hs", gi][:])
 
-        w_grp = const.tile([P, 2, NG, 2], F32, align_bytes=64)
-        w_codes = const.tile([P, 2 * NG], U32, align_bytes=64)
-        w_scales = const.tile([P, 2 * NG], U8, align_bytes=64)
-        for j in range(6):
-            w_ps = psum.tile([P, 4, P], F32, tag=("A0", "A1", "AC")[j % 3], name="w_ps")
+        def w_pe(j, tag):
+            w_ps = psum.tile([P, 4, P], F32, tag=tag, name="w_ps")
+            ps_t["w", j] = w_ps
             ww = w_raw[:, j, :].bitcast(F32)
             for q in range(4):
                 nc.tensor.transpose(w_ps[:, q, :], ww[:, P * q:P * q + P], ident_f[:])
-            src = w_ps[:].rearrange("p (g u) r -> p g r u", g=2)
-            if j % 2 == 0:
-                nc.scalar.copy(out=w_grp[:, :, P * j:P * j + P, :], in_=src)
-            else:
-                nc.vector.tensor_copy(out=w_grp[:, :, P * j:P * j + P, :], in_=src)
-        wg_bf = w_grp[:].rearrange("p g n u -> p (g n u)").bitcast(BF16)
-        nc.vector.quantize_mx(out=w_codes[:, 0:1024].bitcast(FP8X4), scales=w_scales[:, 0:1024], in_=wg_bf[:, 0:4096])
-        nc.vector.quantize_mx(out=w_codes[:, 1024:1536].bitcast(FP8X4), scales=w_scales[:, 1024:1536], in_=wg_bf[:, 4096:6144])
 
-        xg_t = {}
-        xq_t = {}
-        pl_t = {}
-        pb_t = {}
-        mx_t = {}
-        g4_t = {}
-        out_t = {}
+        def w_ev(j, eng):
+            copy_out(eng, w_grp[:, :, P * j:P * j + P, :], ps_t["w", j][:].rearrange("p (g u) r -> p g r u", g=2))
 
-        def x_transposes(k):
-            xg = qpool.tile([P, 2, 2, P, 2], F32, align_bytes=64, name="xg")
-            xg_t[k] = xg
-            for i in range(2):
-                t = 2 * k + i
-                xt = psum.tile([P, 4, P], F32, tag="X%d" % i, name="xt")
-                xw = x_tiles[t // 4][:, t % 4, :].bitcast(F32)
-                for q in range(4):
-                    nc.tensor.transpose(xt[:, q, :], xw[:, P * q:P * q + P], ident_f[:])
-                nc.scalar.copy(out=xg[:, i], in_=xt[:].rearrange("p (g u) r -> p g r u", g=2))
+        def w_quant(a):
+            for g in range(2):
+                lo = g * NG + 256 * a
+                nc.vector.quantize_mx(
+                    out=w_codes[:, lo:lo + 256].bitcast(FP8X4), scales=w_scales[:, lo:lo + 256],
+                    in_=w_grp[:, g, 256 * a:256 * a + 256, :].rearrange("p n u -> p (n u)").bitcast(BF16),
+                )
+
+        def x_pe(t, tag):
+            xt = psum.tile([P, 4, P], F32, tag=tag, name="xt")
+            ps_t["x", t] = xt
+            xw = xp_t[t // 2][:, t % 2, :].bitcast(F32)
+            for q in range(4):
+                nc.tensor.transpose(xt[:, q, :], xw[:, P * q:P * q + P], ident_f[:])
+
+        def x_ev(t, eng):
+            k = t // 2
+            if t % 2 == 0:
+                xg_new = qpool.tile([P, 2, 2, P, 2], F32, align_bytes=64, name="xg")
+                xg_t[k] = xg_new
+            copy_out(eng, xg_t[k][:, t % 2], ps_t["x", t][:].rearrange("p (g u) r -> p g r u", g=2))
 
         def quantise(k):
             xc = qpool.tile([P, 512], U32, align_bytes=64, name="xc")
@@ -171,14 +172,14 @@ def tile_share_lstm_cell_t_kernel(
             p0 = psum.tile([P, 512], F32, tag="P0", name="p0")
             p1 = psum.tile([P, 512], F32, tag="P1", name="p1")
             pc = psum.tile([P, 512], F32, tag="PC", name="pc")
-            pl_t[k] = (p0, p1, pc)
+            ps_t["pl", k] = (p0, p1, pc)
             nc.tensor.matmul(out=p0[:], lhsT=hsT[:, gi, 0, tt, :], rhs=wT[:, 0:512], start=True, stop=True)
             nc.tensor.matmul(out=p1[:], lhsT=hsT[:, gi, 0, tt + 1, :], rhs=wT[:, 0:512], start=True, stop=True)
             nc.tensor.matmul(out=pc[:, 0:256], lhsT=hsT[:, gi, 1, tt, :], rhs=wT[:, 512:768], start=True, stop=True)
             nc.tensor.matmul(out=pc[:, 256:512], lhsT=hsT[:, gi, 1, tt + 1, :], rhs=wT[:, 512:768], start=True, stop=True)
 
         def add_bias(k):
-            p0, p1, pc = pl_t[k]
+            p0, p1, pc = ps_t["pl", k]
             pb = pbpool.tile([P, 2, NG], F32, name="pb")
             pb_t[k] = pb
             nc.vector.tensor_tensor(out=pb[:, 0, 0:512], in0=p0[:], in1=bias_bc[:, 0:512], op=ALU.add)
@@ -193,7 +194,7 @@ def tile_share_lstm_cell_t_kernel(
             a0 = psum.tile([P, 512], F32, tag="A0", name="a0")
             a1 = psum.tile([P, 512], F32, tag="A1", name="a1")
             ac = psum.tile([P, 512], F32, tag="AC", name="ac")
-            mx_t[k] = (a0, a1, ac)
+            ps_t["mx", k] = (a0, a1, ac)
             for i in range(2):
                 dst = (a0, a1)[i]
                 for g in range(2):
@@ -219,7 +220,7 @@ def tile_share_lstm_cell_t_kernel(
                 g4_new = gpool.tile([P, 4, NG], F32, name="g4")
                 g4_t[gi] = g4_new
             g4 = g4_t[gi]
-            a0, a1, ac = mx_t[k]
+            a0, a1, ac = ps_t["mx", k]
             pb = pb_t[k]
             nc.vector.tensor_tensor(out=g4[:, tt, 0:512], in0=a0[:], in1=pb[:, 0, 0:512], op=ALU.add)
             nc.vector.tensor_tensor(out=g4[:, tt + 1, 0:512], in0=a1[:], in1=pb[:, 1, 0:512], op=ALU.add)
@@ -247,10 +248,12 @@ def tile_share_lstm_cell_t_kernel(
             nc.gpsimd.tensor_tensor(out=g4[:, :, 384:512], in0=g4[:, :, 0:128], in1=g4[:, :, 384:512], op=ALU.mult)
             nc.gpsimd.tensor_tensor(out=g4[:, :, 0:128], in0=g4[:, :, 128:256], in1=g4[:, :, 384:512], op=ALU.add)
 
-        def cell_scalar(gi, tt):
+        def cell_scalar(t):
+            gi = t // 4
+            tt = t % 4
             g4 = g4_t[gi]
             oc = out_t[gi][1]
-            m = m32[:, 4 * gi + tt:4 * gi + tt + 1]
+            m = m32[:, t:t + 1]
             nc.scalar.activation(out=g4[:, tt, 128:256], in_=g4[:, tt, 0:128], func=ACT.Tanh, scale=m)
             nc.scalar.activation(out=oc[:, tt, :], in_=g4[:, tt, 0:128], func=ACT.Copy, scale=m)
             nc.scalar.activation(out=g4[:, tt, 384:512], in_=g4[:, tt, 128:256], func=ACT.Copy, scale=m)
@@ -265,76 +268,142 @@ def tile_share_lstm_cell_t_kernel(
                 in1=g4[:, :, 384:512].unsqueeze(2).to_broadcast([P, 4, 2, H]), op=ALU.mult,
             )
 
-        def cell_vector(gi, tt):
+        def cell_vector(t):
+            gi = t // 4
+            tt = t % 4
             g4 = g4_t[gi]
-            oh, oc, os_ = out_t[gi]
-            t = 4 * gi + tt
+            oc = out_t[gi][1]
             m = m32[:, t:t + 1]
             nc.vector.scalar_tensor_tensor(out=g4[:, tt, 128:256], in0=c_sb[:, t, :], scalar=m, in1=g4[:, tt, 128:256], op0=ALU.mult, op1=ALU.mult)
             nc.vector.scalar_tensor_tensor(out=g4[:, tt, 384:512], in0=g4[:, tt, 384:512], scalar=m, in1=g4[:, tt, 0:128], op0=ALU.mult, op1=ALU.mult)
             nc.vector.tensor_tensor(out=oc[:, tt, :], in0=g4[:, tt, 128:256], in1=g4[:, tt, 384:512], op=ALU.add)
             nc.scalar.activation(out=g4[:, tt, 0:128], in_=oc[:, tt, :], func=ACT.Tanh)
 
-        def outputs_vector(gi, tt):
+        def outputs_vector(t):
+            gi = t // 4
+            tt = t % 4
             g4 = g4_t[gi]
             oh, oc, os_ = out_t[gi]
-            m = m32[:, 4 * gi + tt:4 * gi + tt + 1]
+            m = m32[:, t:t + 1]
             nc.vector.scalar_tensor_tensor(out=oh[:, tt, :], in0=g4[:, tt, 0:128], scalar=m, in1=g4[:, tt, 256:384], op0=ALU.mult, op1=ALU.mult)
             nc.vector.scalar_tensor_tensor(
                 out=os_[:, :, tt, :], in0=g4[:, tt, 0:128].unsqueeze(1).to_broadcast([P, 2, H]), scalar=m,
                 in1=g4[:, tt, 512:768].rearrange("p (k c) -> p k c", k=2), op0=ALU.mult, op1=ALU.mult,
             )
 
-        def store(gi, which):
+        def store(gi, which, lo, n):
             oh, oc, os_ = out_t[gi]
-            src = (oh[:], oc[:], os_[:, 0], os_[:, 1])[which]
-            nc.sync.dma_start(out=outs[which][:, 4 * gi:4 * gi + 4, :], in_=src)
+            src = (oh, oc, os_[:, 0], os_[:, 1])[which]
+            nc.sync.dma_start(out=outs[which][:, 4 * gi + lo:4 * gi + lo + n, :], in_=src[:, lo:lo + n, :])
+
+        wt_ps = psum.tile([P, 6, H], BF16, tag="X0", name="wt_ps")
+        for j in range(6):
+            nc.tensor.transpose(wt_ps[:, j, :], whh_raw[:, j, :], ident_b[:])
+        nc.scalar.copy(out=wT[:], in_=wt_ps[:].rearrange("p j k -> p (j k)"))
+        hs_pe(0, "X1")
+        hs_ev(0, "S")
+        b_ps0 = psum.tile([P, 512], F32, tag="A0", name="b_ps0")
+        b_ps1 = psum.tile([P, 512], F32, tag="AC", name="b_ps1")
+        nc.tensor.matmul(out=b_ps0[:], lhsT=ones[:], rhs=braw[:, 0:512], start=True, stop=True)
+        nc.tensor.matmul(out=b_ps1[:, 0:256], lhsT=ones[:], rhs=braw[:, 512:768], start=True, stop=True)
+        nc.scalar.copy(out=bias_bc[:, 0:512], in_=b_ps0[:])
+        nc.scalar.copy(out=bias_bc[:, 512:768], in_=b_ps1[:, 0:256])
+        plain(0)
+        add_bias(0)
+        w_tags = ("A1", "A0", "AC", "A1", "A0", "AC")
+        for a in range(2):
+            for j in (2 * a, 2 * a + 1):
+                w_pe(j, w_tags[j])
+                w_ev(j, "S")
+            w_quant(a)
+        x_pe(0, "X0")
+        x_ev(0, "S")
+        x_pe(1, "X1")
+        x_ev(1, "S")
+        quantise(0)
+        for j in (4, 5):
+            w_pe(j, w_tags[j])
+            w_ev(j, "S")
+        w_quant(2)
+        hs_pe(1, "X0")
+        hs_ev(1, "S")
+        x_pe(2, "X1")
+        x_ev(2, "S")
+        x_pe(3, "X0")
+        x_ev(3, "S")
+        mx(0)
+        for k in range(1, LA + 1):
+            plain(k)
+            if k < LA:
+                add_bias(k)
+        quantise(1)
+        nc.vector.tensor_copy(out=m32[:], in_=m_bf[:])
+        x_pe(4, "X1")
+        x_ev(4, "S")
+        x_pe(5, "X0")
+        x_ev(5, "S")
 
         NGP = NGROUP - V_GROUPS
-        for j in range(-3, NPAIR + 8):
-            if 0 <= j + 1 < NPAIR:
+
+        def gp_group(j, off):
+            if (j - off) % 2 == 0 and 0 <= (j - off) // 2 < NGP:
+                return (j - off) // 2
+            return -1
+
+        for j in range(NPAIR + 8):
+            kk = j + LA + 2
+            do_hs = kk % 2 == 0 and 2 <= kk // 2 < NGROUP
+            if do_hs:
+                hs_pe(kk // 2, "X1")
+            if j + 1 < NPAIR:
                 mx(j + 1)
-            if 0 <= j + 3 < NPAIR:
-                if (j + 3) % 2 == 0 and (j + 3) // 2 + 2 < NGROUP and (j + 3) // 2 + 2 >= 4:
-                    load_x((j + 3) // 2 + 2)
-                x_transposes(j + 3)
-            kk = j + 2 + LA
-            if kk % 2 == 0 and 2 <= kk // 2 < NGROUP:
-                hs_transposes(kk // 2, 1)
-            if 0 <= j + 1 + LA < NPAIR:
-                plain(j + 1 + LA)
-            if 0 <= j < NPAIR:
+            if j < NPAIR:
                 add_mx(j)
-            if 0 <= j + 2 < NPAIR:
-                quantise(j + 2)
-            if 0 <= j + LA < NPAIR:
-                add_bias(j + LA)
+            if j + QL < NPAIR:
+                quantise(j + QL)
             if 0 <= j - 1 < NPAIR:
                 gate_functions(j - 1)
-            if (j - 3) % 2 == 0 and 0 <= (j - 3) // 2 < NGP:
-                out_tiles((j - 3) // 2)
-                cell_sum_gpsimd((j - 3) // 2)
-            if (j - 4) % 2 == 0 and 0 <= (j - 4) // 2 < NGP:
-                cell_scalar((j - 4) // 2, 0)
-                cell_scalar((j - 4) // 2, 1)
-            if (j - 5) % 2 == 0 and 0 <= (j - 5) // 2 < NGP:
-                cell_scalar((j - 5) // 2, 2)
-                cell_scalar((j - 5) // 2, 3)
-                store((j - 5) // 2, 1)
-            if (j - 6) % 2 == 0 and 0 <= (j - 6) // 2 < NGP:
-                outputs_gpsimd((j - 6) // 2)
-                store((j - 6) // 2, 0)
-                store((j - 6) // 2, 2)
-                store((j - 6) // 2, 3)
-            if 0 <= j - 2 < NPAIR and (j - 2) // 2 >= NGP:
-                gi = (j - 2) // 2
-                tt = 2 * ((j - 2) % 2)
-                if tt == 0:
-                    out_tiles(gi)
-                cell_vector(gi, tt)
-                cell_vector(gi, tt + 1)
-                outputs_vector(gi, tt)
-                outputs_vector(gi, tt + 1)
-                if tt == 2:
-                    for which in (1, 0, 2, 3):
-                        store(gi, which)
+            if do_hs:
+                hs_ev(kk // 2, "S")
+            g = gp_group(j, 3)
+            if g >= 0:
+                out_tiles(g)
+                cell_sum_gpsimd(g)
+            g = gp_group(j, 4)
+            if g >= 0:
+                cell_scalar(4 * g)
+                cell_scalar(4 * g + 1)
+            g = gp_group(j, 5)
+            if g >= 0:
+                cell_scalar(4 * g + 2)
+                cell_scalar(4 * g + 3)
+                store(g, 1, 0, 4)
+            g = gp_group(j, 6)
+            if g >= 0:
+                outputs_gpsimd(g)
+                store(g, 0, 0, 4)
+                store(g, 2, 0, 4)
+                store(g, 3, 0, 4)
+            if j + XL < NPAIR:
+                if j + XL + 5 < NPAIR:
+                    load_x(j + XL + 5)
+                x_pe(2 * (j + XL), "X0")
+                x_pe(2 * (j + XL) + 1, "X1")
+                x_ev(2 * (j + XL), "S")
+                x_ev(2 * (j + XL) + 1, "S")
+            if j + LA + 1 < NPAIR:
+                plain(j + LA + 1)
+            if j + LA < NPAIR:
+                add_bias(j + LA)
+            k1 = j - 1
+            k2 = j - 2
+            if 0 <= k1 < NPAIR and k1 // 2 >= NGP:
+                if k1 % 2 == 0:
+                    out_tiles(k1 // 2)
+                cell_vector(2 * k1)
+                cell_vector(2 * k1 + 1)
+            if 0 <= k2 < NPAIR and k2 // 2 >= NGP:
+                outputs_vector(2 * k2)
+                outputs_vector(2 * k2 + 1)
+                for which in (1, 0, 2, 3):
+                    store(k2 // 2, which, 2 * (k2 % 2), 2)

@@ -23,7 +23,8 @@ LA = 1
 XL = 3
 QL = 2
 PINNED = True
-V_GROUPS = 1
+NG_SUM = 7
+NG_OUT = 5
 
 FLOPS = 2 * B * (D_IN * NG + H * 512 + H * 256)
 BYTES = 2 * (B * D_IN + 3 * B * H + B + NG * D_IN + 768 * H + 2 * NG) + 4 * 4 * B * H
@@ -256,7 +257,8 @@ def tile_share_lstm_cell_t_kernel(
             m = m32[:, t:t + 1]
             nc.scalar.activation(out=g4[:, tt, 128:256], in_=g4[:, tt, 0:128], func=ACT.Tanh, scale=m)
             nc.scalar.activation(out=oc[:, tt, :], in_=g4[:, tt, 0:128], func=ACT.Copy, scale=m)
-            nc.scalar.activation(out=g4[:, tt, 384:512], in_=g4[:, tt, 128:256], func=ACT.Copy, scale=m)
+            if gi < NG_OUT:
+                nc.scalar.activation(out=g4[:, tt, 384:512], in_=g4[:, tt, 128:256], func=ACT.Copy, scale=m)
 
         def outputs_gpsimd(gi):
             g4 = g4_t[gi]
@@ -277,7 +279,7 @@ def tile_share_lstm_cell_t_kernel(
             nc.vector.scalar_tensor_tensor(out=g4[:, tt, 128:256], in0=c_sb[:, t, :], scalar=m, in1=g4[:, tt, 128:256], op0=ALU.mult, op1=ALU.mult)
             nc.vector.scalar_tensor_tensor(out=g4[:, tt, 384:512], in0=g4[:, tt, 384:512], scalar=m, in1=g4[:, tt, 0:128], op0=ALU.mult, op1=ALU.mult)
             nc.vector.tensor_tensor(out=oc[:, tt, :], in0=g4[:, tt, 128:256], in1=g4[:, tt, 384:512], op=ALU.add)
-            nc.scalar.activation(out=g4[:, tt, 0:128], in_=oc[:, tt, :], func=ACT.Tanh)
+            nc.scalar.activation(out=g4[:, tt, 128:256], in_=oc[:, tt, :], func=ACT.Tanh)
 
         def outputs_vector(t):
             gi = t // 4
@@ -285,9 +287,9 @@ def tile_share_lstm_cell_t_kernel(
             g4 = g4_t[gi]
             oh, oc, os_ = out_t[gi]
             m = m32[:, t:t + 1]
-            nc.vector.scalar_tensor_tensor(out=oh[:, tt, :], in0=g4[:, tt, 0:128], scalar=m, in1=g4[:, tt, 256:384], op0=ALU.mult, op1=ALU.mult)
+            nc.vector.scalar_tensor_tensor(out=oh[:, tt, :], in0=g4[:, tt, 128:256], scalar=m, in1=g4[:, tt, 256:384], op0=ALU.mult, op1=ALU.mult)
             nc.vector.scalar_tensor_tensor(
-                out=os_[:, :, tt, :], in0=g4[:, tt, 0:128].unsqueeze(1).to_broadcast([P, 2, H]), scalar=m,
+                out=os_[:, :, tt, :], in0=g4[:, tt, 128:256].unsqueeze(1).to_broadcast([P, 2, H]), scalar=m,
                 in1=g4[:, tt, 512:768].rearrange("p (k c) -> p k c", k=2), op0=ALU.mult, op1=ALU.mult,
             )
 
@@ -306,24 +308,26 @@ def tile_share_lstm_cell_t_kernel(
         b_ps1 = psum.tile([P, 512], F32, tag="AC", name="b_ps1")
         nc.tensor.matmul(out=b_ps0[:], lhsT=ones[:], rhs=braw[:, 0:512], start=True, stop=True)
         nc.tensor.matmul(out=b_ps1[:, 0:256], lhsT=ones[:], rhs=braw[:, 512:768], start=True, stop=True)
-        nc.scalar.copy(out=bias_bc[:, 0:512], in_=b_ps0[:])
-        nc.scalar.copy(out=bias_bc[:, 512:768], in_=b_ps1[:, 0:256])
+        nc.vector.tensor_copy(out=bias_bc[:, 0:512], in_=b_ps0[:])
+        nc.vector.tensor_copy(out=bias_bc[:, 512:768], in_=b_ps1[:, 0:256])
         plain(0)
         add_bias(0)
-        w_tags = ("A1", "A0", "AC", "A1", "A0", "AC")
+        w_tags = ("A1", "A0", "AC", "X0", "A1", "A0")
         for a in range(2):
-            for j in (2 * a, 2 * a + 1):
-                w_pe(j, w_tags[j])
-                w_ev(j, "S")
+            w_pe(2 * a, w_tags[2 * a])
+            w_ev(2 * a, "S")
+            w_pe(2 * a + 1, w_tags[2 * a + 1])
+            w_ev(2 * a + 1, "V")
             w_quant(a)
-        x_pe(0, "X0")
+        x_pe(0, "X1")
         x_ev(0, "S")
-        x_pe(1, "X1")
-        x_ev(1, "S")
+        x_pe(1, "AC")
+        x_ev(1, "V")
         quantise(0)
-        for j in (4, 5):
-            w_pe(j, w_tags[j])
-            w_ev(j, "S")
+        w_pe(4, w_tags[4])
+        w_ev(4, "S")
+        w_pe(5, w_tags[5])
+        w_ev(5, "V")
         w_quant(2)
         hs_pe(1, "X0")
         hs_ev(1, "S")
@@ -332,21 +336,16 @@ def tile_share_lstm_cell_t_kernel(
         x_pe(3, "X0")
         x_ev(3, "S")
         mx(0)
-        for k in range(1, LA + 1):
-            plain(k)
-            if k < LA:
-                add_bias(k)
-        quantise(1)
+        plain(1)
         nc.vector.tensor_copy(out=m32[:], in_=m_bf[:])
+        quantise(1)
         x_pe(4, "X1")
         x_ev(4, "S")
         x_pe(5, "X0")
         x_ev(5, "S")
 
-        NGP = NGROUP - V_GROUPS
-
-        def gp_group(j, off):
-            if (j - off) % 2 == 0 and 0 <= (j - off) // 2 < NGP:
+        def group_at(j, off, limit):
+            if (j - off) % 2 == 0 and 0 <= (j - off) // 2 < limit:
                 return (j - off) // 2
             return -1
 
@@ -365,20 +364,20 @@ def tile_share_lstm_cell_t_kernel(
                 gate_functions(j - 1)
             if do_hs:
                 hs_ev(kk // 2, "S")
-            g = gp_group(j, 3)
+            g = group_at(j, 3, NG_SUM)
             if g >= 0:
                 out_tiles(g)
                 cell_sum_gpsimd(g)
-            g = gp_group(j, 4)
+            g = group_at(j, 4, NG_SUM)
             if g >= 0:
                 cell_scalar(4 * g)
                 cell_scalar(4 * g + 1)
-            g = gp_group(j, 5)
+            g = group_at(j, 5, NG_SUM)
             if g >= 0:
                 cell_scalar(4 * g + 2)
                 cell_scalar(4 * g + 3)
                 store(g, 1, 0, 4)
-            g = gp_group(j, 6)
+            g = group_at(j, 6, NG_OUT)
             if g >= 0:
                 outputs_gpsimd(g)
                 store(g, 0, 0, 4)
@@ -395,14 +394,21 @@ def tile_share_lstm_cell_t_kernel(
                 plain(j + LA + 1)
             if j + LA < NPAIR:
                 add_bias(j + LA)
+            g = group_at(j, 6, NG_SUM)
+            if g >= NG_OUT:
+                for tt in range(4):
+                    outputs_vector(4 * g + tt)
+                store(g, 0, 0, 4)
+                store(g, 2, 0, 4)
+                store(g, 3, 0, 4)
             k1 = j - 1
             k2 = j - 2
-            if 0 <= k1 < NPAIR and k1 // 2 >= NGP:
+            if 0 <= k1 < NPAIR and k1 // 2 >= NG_SUM:
                 if k1 % 2 == 0:
                     out_tiles(k1 // 2)
                 cell_vector(2 * k1)
                 cell_vector(2 * k1 + 1)
-            if 0 <= k2 < NPAIR and k2 // 2 >= NGP:
+            if 0 <= k2 < NPAIR and k2 // 2 >= NG_SUM:
                 outputs_vector(2 * k2)
                 outputs_vector(2 * k2 + 1)
                 for which in (1, 0, 2, 3):

@@ -15,14 +15,15 @@ P = 128
 B = 4096
 D_IN = 1024
 H = 128
-NG = 768
+NG = 6 * H
+NH = 4 * H
 NT = B // P
 NPAIR = NT // 2
 NGROUP = NT // 4
-LA = 1
-XL = 3
-QL = 2
-PINNED = True
+
+X_AHEAD = 3
+QUANT_AHEAD = 2
+PLAIN_AHEAD = 1
 NG_SUM = 7
 NG_OUT = 5
 
@@ -39,12 +40,10 @@ def tile_share_lstm_cell_t_kernel(
         const = ctx.enter_context(tc.tile_pool(name="const", bufs=1))
         xpool = ctx.enter_context(tc.tile_pool(name="xpool", bufs=8))
         qpool = ctx.enter_context(tc.tile_pool(name="qpool", bufs=3))
-        pbpool = ctx.enter_context(tc.tile_pool(name="pbpool", bufs=LA + 1))
+        pbpool = ctx.enter_context(tc.tile_pool(name="pbpool", bufs=PLAIN_AHEAD + 1))
         gpool = ctx.enter_context(tc.tile_pool(name="gpool", bufs=5))
         opool = ctx.enter_context(tc.tile_pool(name="opool", bufs=3))
         psum = ctx.enter_context(tc.psum_pool(name="psum", bufs=1))
-        if PINNED:
-            ctx.enter_context(tc.manual_schedule())
 
         xv = x_in.rearrange("(p t) k -> p t k", t=NT)
         hv = h_minors.rearrange("(p t) k -> p t k", t=NT)
@@ -71,32 +70,29 @@ def tile_share_lstm_cell_t_kernel(
         w_codes = const.tile([P, 2 * NG], U32, align_bytes=64)
         w_scales = const.tile([P, 2 * NG], U8, align_bytes=64)
 
-        xp_t = {}
-        ps_t = {}
-        xg_t = {}
-        xq_t = {}
-        pb_t = {}
-        g4_t = {}
-        out_t = {}
+        x_of = {}
+        bank = {}
+        xg_of = {}
+        xq_of = {}
+        pb_of = {}
+        g4_of = {}
+        out_of = {}
+
+        scalar_copy = nc.scalar.copy
+        vector_copy = nc.vector.tensor_copy
 
         def load_x(k):
             x_sb = xpool.tile([P, 2, D_IN], BF16, name="x_sb")
             nc.sync.dma_start(out=x_sb[:], in_=xv[:, 2 * k:2 * k + 2, :])
-            xp_t[k] = x_sb
-
-        def copy_out(eng, out, in_):
-            if eng == "V":
-                nc.vector.tensor_copy(out=out, in_=in_)
-            else:
-                nc.scalar.copy(out=out, in_=in_)
+            x_of[k] = x_sb
 
         nc.vector.memset(braw[:], 0.0)
         nc.vector.memset(ones[:], 1.0)
         make_identity(nc, ident_b[:])
         make_identity(nc, ident_f[:])
         nc.scalar.dma_start(out=braw[0:1, :], in_=bias_ih.unsqueeze(0))
-        nc.scalar.dma_start(out=braw[1:2, 0:512], in_=bias_hh.unsqueeze(0))
-        nc.scalar.dma_start(out=braw[1:2, 512:768], in_=bias_sh.unsqueeze(0))
+        nc.scalar.dma_start(out=braw[1:2, 0:NH], in_=bias_hh.unsqueeze(0))
+        nc.scalar.dma_start(out=braw[1:2, NH:NG], in_=bias_sh.unsqueeze(0))
         nc.sync.dma_start(out=whh_raw[:, 0:4, :], in_=weight_hh.rearrange("(j p) k -> p j k", p=P))
         nc.sync.dma_start(out=whh_raw[:, 4:6, :], in_=weight_sh.rearrange("(j p) k -> p j k", p=P))
         nc.sync.dma_start(out=h_sb[:, 0:8, :], in_=hv[:, 0:8, :])
@@ -115,28 +111,34 @@ def tile_share_lstm_cell_t_kernel(
         for k in range(4, 8):
             load_x(k)
 
-        def hs_pe(gi, tag):
+        def hs_transposes(gi, tag):
             hs_ps = psum.tile([P, 2, 4, H], BF16, tag=tag, name="hs_ps")
-            ps_t["hs", gi] = hs_ps
+            bank["hs", gi] = hs_ps
             for tt in range(4):
                 nc.tensor.transpose(hs_ps[:, 0, tt, :], h_sb[:, 4 * gi + tt, :], ident_b[:])
             for tt in range(4):
                 nc.tensor.transpose(hs_ps[:, 1, tt, :], s_sb[:, 4 * gi + tt, :], ident_b[:])
 
-        def hs_ev(gi, eng):
-            copy_out(eng, hsT[:, gi], ps_t["hs", gi][:])
+        def hs_copy(gi):
+            scalar_copy(out=hsT[:, gi], in_=bank["hs", gi][:])
 
-        def w_pe(j, tag):
-            w_ps = psum.tile([P, 4, P], F32, tag=tag, name="w_ps")
-            ps_t["w", j] = w_ps
-            ww = w_raw[:, j, :].bitcast(F32)
+        def word_transposes(rows, tag, name):
+            planes = psum.tile([P, 4, P], F32, tag=tag, name=name)
+            words = rows.bitcast(F32)
             for q in range(4):
-                nc.tensor.transpose(w_ps[:, q, :], ww[:, P * q:P * q + P], ident_f[:])
+                nc.tensor.transpose(planes[:, q, :], words[:, P * q:P * q + P], ident_f[:])
+            return planes
 
-        def w_ev(j, eng):
-            copy_out(eng, w_grp[:, :, P * j:P * j + P, :], ps_t["w", j][:].rearrange("p (g u) r -> p g r u", g=2))
+        def regrouped(planes):
+            return planes[:].rearrange("p (g u) r -> p g r u", g=2)
 
-        def w_quant(a):
+        def w_transposes(j, tag):
+            bank["w", j] = word_transposes(w_raw[:, j, :], tag, "w_ps")
+
+        def w_copy(j, copy):
+            copy(out=w_grp[:, :, P * j:P * j + P, :], in_=regrouped(bank["w", j]))
+
+        def w_quantise(a):
             for g in range(2):
                 lo = g * NG + 256 * a
                 nc.vector.quantize_mx(
@@ -144,65 +146,61 @@ def tile_share_lstm_cell_t_kernel(
                     in_=w_grp[:, g, 256 * a:256 * a + 256, :].rearrange("p n u -> p (n u)").bitcast(BF16),
                 )
 
-        def x_pe(t, tag):
-            xt = psum.tile([P, 4, P], F32, tag=tag, name="xt")
-            ps_t["x", t] = xt
-            xw = xp_t[t // 2][:, t % 2, :].bitcast(F32)
-            for q in range(4):
-                nc.tensor.transpose(xt[:, q, :], xw[:, P * q:P * q + P], ident_f[:])
+        def x_transposes(t, tag):
+            bank["x", t] = word_transposes(x_of[t // 2][:, t % 2, :], tag, "xt")
 
-        def x_ev(t, eng):
+        def x_copy(t, copy):
             k = t // 2
             if t % 2 == 0:
                 xg_new = qpool.tile([P, 2, 2, P, 2], F32, align_bytes=64, name="xg")
-                xg_t[k] = xg_new
-            copy_out(eng, xg_t[k][:, t % 2], ps_t["x", t][:].rearrange("p (g u) r -> p g r u", g=2))
+                xg_of[k] = xg_new
+            copy(out=xg_of[k][:, t % 2], in_=regrouped(bank["x", t]))
 
         def quantise(k):
             xc = qpool.tile([P, 512], U32, align_bytes=64, name="xc")
             xs = qpool.tile([P, 512], U8, align_bytes=64, name="xs")
-            xq_t[k] = (xc, xs)
+            xq_of[k] = (xc, xs)
             nc.vector.quantize_mx(
                 out=xc[:].bitcast(FP8X4), scales=xs[:],
-                in_=xg_t[k][:].rearrange("p t g r u -> p (t g r u)").bitcast(BF16),
+                in_=xg_of[k][:].rearrange("p t g r u -> p (t g r u)").bitcast(BF16),
             )
 
-        def plain(k):
+        def plain_products(k):
             gi = k // 2
             tt = 2 * (k % 2)
             p0 = psum.tile([P, 512], F32, tag="P0", name="p0")
             p1 = psum.tile([P, 512], F32, tag="P1", name="p1")
             pc = psum.tile([P, 512], F32, tag="PC", name="pc")
-            ps_t["pl", k] = (p0, p1, pc)
-            nc.tensor.matmul(out=p0[:], lhsT=hsT[:, gi, 0, tt, :], rhs=wT[:, 0:512], start=True, stop=True)
-            nc.tensor.matmul(out=p1[:], lhsT=hsT[:, gi, 0, tt + 1, :], rhs=wT[:, 0:512], start=True, stop=True)
-            nc.tensor.matmul(out=pc[:, 0:256], lhsT=hsT[:, gi, 1, tt, :], rhs=wT[:, 512:768], start=True, stop=True)
-            nc.tensor.matmul(out=pc[:, 256:512], lhsT=hsT[:, gi, 1, tt + 1, :], rhs=wT[:, 512:768], start=True, stop=True)
+            bank["plain", k] = (p0, p1, pc)
+            nc.tensor.matmul(out=p0[:], lhsT=hsT[:, gi, 0, tt, :], rhs=wT[:, 0:NH], start=True, stop=True)
+            nc.tensor.matmul(out=p1[:], lhsT=hsT[:, gi, 0, tt + 1, :], rhs=wT[:, 0:NH], start=True, stop=True)
+            nc.tensor.matmul(out=pc[:, 0:256], lhsT=hsT[:, gi, 1, tt, :], rhs=wT[:, NH:NG], start=True, stop=True)
+            nc.tensor.matmul(out=pc[:, 256:512], lhsT=hsT[:, gi, 1, tt + 1, :], rhs=wT[:, NH:NG], start=True, stop=True)
 
         def add_bias(k):
-            p0, p1, pc = ps_t["pl", k]
+            p0, p1, pc = bank["plain", k]
             pb = pbpool.tile([P, 2, NG], F32, name="pb")
-            pb_t[k] = pb
-            nc.vector.tensor_tensor(out=pb[:, 0, 0:512], in0=p0[:], in1=bias_bc[:, 0:512], op=ALU.add)
-            nc.vector.tensor_tensor(out=pb[:, 1, 0:512], in0=p1[:], in1=bias_bc[:, 0:512], op=ALU.add)
+            pb_of[k] = pb
+            nc.vector.tensor_tensor(out=pb[:, 0, 0:NH], in0=p0[:], in1=bias_bc[:, 0:NH], op=ALU.add)
+            nc.vector.tensor_tensor(out=pb[:, 1, 0:NH], in0=p1[:], in1=bias_bc[:, 0:NH], op=ALU.add)
             nc.vector.tensor_tensor(
-                out=pb[:, :, 512:768], in0=pc[:].rearrange("p (t n) -> p t n", t=2),
-                in1=bias_bc[:, 512:768].unsqueeze(1).to_broadcast([P, 2, 256]), op=ALU.add,
+                out=pb[:, :, NH:NG], in0=pc[:].rearrange("p (t n) -> p t n", t=2),
+                in1=bias_bc[:, NH:NG].unsqueeze(1).to_broadcast([P, 2, 256]), op=ALU.add,
             )
 
-        def mx(k):
-            xc, xs = xq_t[k]
+        def mx_products(k):
+            xc, xs = xq_of[k]
             a0 = psum.tile([P, 512], F32, tag="A0", name="a0")
             a1 = psum.tile([P, 512], F32, tag="A1", name="a1")
             ac = psum.tile([P, 512], F32, tag="AC", name="ac")
-            ps_t["mx", k] = (a0, a1, ac)
+            bank["mx", k] = (a0, a1, ac)
             for i in range(2):
                 dst = (a0, a1)[i]
                 for g in range(2):
                     lo = (2 * i + g) * P
                     nc.tensor.matmul_mx(
                         out=dst[:], lhsT=xc[:, lo:lo + P].bitcast(FP8X4), lhsT_scale=xs[:, lo:lo + P],
-                        rhs=w_codes[:, g * NG:g * NG + 512].bitcast(FP8X4), rhs_scale=w_scales[:, g * NG:g * NG + 512],
+                        rhs=w_codes[:, g * NG:g * NG + NH].bitcast(FP8X4), rhs_scale=w_scales[:, g * NG:g * NG + NH],
                         start=(g == 0), stop=(g == 1),
                     )
             for i in range(2):
@@ -210,7 +208,7 @@ def tile_share_lstm_cell_t_kernel(
                     lo = (2 * i + g) * P
                     nc.tensor.matmul_mx(
                         out=ac[:, 256 * i:256 * i + 256], lhsT=xc[:, lo:lo + P].bitcast(FP8X4), lhsT_scale=xs[:, lo:lo + P],
-                        rhs=w_codes[:, g * NG + 512:g * NG + 768].bitcast(FP8X4), rhs_scale=w_scales[:, g * NG + 512:g * NG + 768],
+                        rhs=w_codes[:, g * NG + NH:g * NG + NG].bitcast(FP8X4), rhs_scale=w_scales[:, g * NG + NH:g * NG + NG],
                         start=(g == 0), stop=(g == 1),
                     )
 
@@ -219,19 +217,19 @@ def tile_share_lstm_cell_t_kernel(
             tt = 2 * (k % 2)
             if tt == 0:
                 g4_new = gpool.tile([P, 4, NG], F32, name="g4")
-                g4_t[gi] = g4_new
-            g4 = g4_t[gi]
-            a0, a1, ac = ps_t["mx", k]
-            pb = pb_t[k]
-            nc.vector.tensor_tensor(out=g4[:, tt, 0:512], in0=a0[:], in1=pb[:, 0, 0:512], op=ALU.add)
-            nc.vector.tensor_tensor(out=g4[:, tt + 1, 0:512], in0=a1[:], in1=pb[:, 1, 0:512], op=ALU.add)
+                g4_of[gi] = g4_new
+            g4 = g4_of[gi]
+            a0, a1, ac = bank["mx", k]
+            pb = pb_of[k]
+            nc.vector.tensor_tensor(out=g4[:, tt, 0:NH], in0=a0[:], in1=pb[:, 0, 0:NH], op=ALU.add)
+            nc.vector.tensor_tensor(out=g4[:, tt + 1, 0:NH], in0=a1[:], in1=pb[:, 1, 0:NH], op=ALU.add)
             nc.vector.tensor_tensor(
-                out=g4[:, tt:tt + 2, 512:768], in0=ac[:].rearrange("p (t n) -> p t n", t=2),
-                in1=pb[:, :, 512:768], op=ALU.add,
+                out=g4[:, tt:tt + 2, NH:NG], in0=ac[:].rearrange("p (t n) -> p t n", t=2),
+                in1=pb[:, :, NH:NG], op=ALU.add,
             )
 
         def gate_functions(k):
-            g4 = g4_t[k // 2]
+            g4 = g4_of[k // 2]
             tt = 2 * (k % 2)
             nc.scalar.activation(out=g4[:, tt:tt + 2, 0:384], in_=g4[:, tt:tt + 2, 0:384], func=ACT.Sigmoid)
             nc.scalar.activation(out=g4[:, tt:tt + 2, 384:512], in_=g4[:, tt:tt + 2, 384:512], func=ACT.Tanh)
@@ -241,10 +239,10 @@ def tile_share_lstm_cell_t_kernel(
             oh = opool.tile([P, 4, H], F32, name="oh")
             oc = opool.tile([P, 4, H], F32, name="oc")
             os_ = opool.tile([P, 2, 4, H], F32, name="os_")
-            out_t[gi] = (oh, oc, os_)
+            out_of[gi] = (oh, oc, os_)
 
         def cell_sum_gpsimd(gi):
-            g4 = g4_t[gi]
+            g4 = g4_of[gi]
             nc.gpsimd.tensor_tensor(out=g4[:, :, 128:256], in0=g4[:, :, 128:256], in1=c_sb[:, 4 * gi:4 * gi + 4, :], op=ALU.mult)
             nc.gpsimd.tensor_tensor(out=g4[:, :, 384:512], in0=g4[:, :, 0:128], in1=g4[:, :, 384:512], op=ALU.mult)
             nc.gpsimd.tensor_tensor(out=g4[:, :, 0:128], in0=g4[:, :, 128:256], in1=g4[:, :, 384:512], op=ALU.add)
@@ -252,8 +250,8 @@ def tile_share_lstm_cell_t_kernel(
         def cell_scalar(t):
             gi = t // 4
             tt = t % 4
-            g4 = g4_t[gi]
-            oc = out_t[gi][1]
+            g4 = g4_of[gi]
+            oc = out_of[gi][1]
             m = m32[:, t:t + 1]
             nc.scalar.activation(out=g4[:, tt, 128:256], in_=g4[:, tt, 0:128], func=ACT.Tanh, scale=m)
             nc.scalar.activation(out=oc[:, tt, :], in_=g4[:, tt, 0:128], func=ACT.Copy, scale=m)
@@ -261,8 +259,8 @@ def tile_share_lstm_cell_t_kernel(
                 nc.scalar.activation(out=g4[:, tt, 384:512], in_=g4[:, tt, 128:256], func=ACT.Copy, scale=m)
 
         def outputs_gpsimd(gi):
-            g4 = g4_t[gi]
-            oh, oc, os_ = out_t[gi]
+            g4 = g4_of[gi]
+            oh, oc, os_ = out_of[gi]
             nc.gpsimd.tensor_tensor(out=oh[:], in0=g4[:, :, 256:384], in1=g4[:, :, 384:512], op=ALU.mult)
             nc.gpsimd.tensor_tensor(
                 out=os_[:].rearrange("p k t c -> p t k c"),
@@ -273,8 +271,8 @@ def tile_share_lstm_cell_t_kernel(
         def cell_vector(t):
             gi = t // 4
             tt = t % 4
-            g4 = g4_t[gi]
-            oc = out_t[gi][1]
+            g4 = g4_of[gi]
+            oc = out_of[gi][1]
             m = m32[:, t:t + 1]
             nc.vector.scalar_tensor_tensor(out=g4[:, tt, 128:256], in0=c_sb[:, t, :], scalar=m, in1=g4[:, tt, 128:256], op0=ALU.mult, op1=ALU.mult)
             nc.vector.scalar_tensor_tensor(out=g4[:, tt, 384:512], in0=g4[:, tt, 384:512], scalar=m, in1=g4[:, tt, 0:128], op0=ALU.mult, op1=ALU.mult)
@@ -284,8 +282,8 @@ def tile_share_lstm_cell_t_kernel(
         def outputs_vector(t):
             gi = t // 4
             tt = t % 4
-            g4 = g4_t[gi]
-            oh, oc, os_ = out_t[gi]
+            g4 = g4_of[gi]
+            oh, oc, os_ = out_of[gi]
             m = m32[:, t:t + 1]
             nc.vector.scalar_tensor_tensor(out=oh[:, tt, :], in0=g4[:, tt, 128:256], scalar=m, in1=g4[:, tt, 256:384], op0=ALU.mult, op1=ALU.mult)
             nc.vector.scalar_tensor_tensor(
@@ -294,76 +292,76 @@ def tile_share_lstm_cell_t_kernel(
             )
 
         def store(gi, which, lo, n):
-            oh, oc, os_ = out_t[gi]
+            oh, oc, os_ = out_of[gi]
             src = (oh, oc, os_[:, 0], os_[:, 1])[which]
             nc.sync.dma_start(out=outs[which][:, 4 * gi + lo:4 * gi + lo + n, :], in_=src[:, lo:lo + n, :])
 
         wt_ps = psum.tile([P, 6, H], BF16, tag="X0", name="wt_ps")
         for j in range(6):
             nc.tensor.transpose(wt_ps[:, j, :], whh_raw[:, j, :], ident_b[:])
-        nc.scalar.copy(out=wT[:], in_=wt_ps[:].rearrange("p j k -> p (j k)"))
-        hs_pe(0, "X1")
-        hs_ev(0, "S")
+        scalar_copy(out=wT[:], in_=wt_ps[:].rearrange("p j k -> p (j k)"))
+        hs_transposes(0, "X1")
+        hs_copy(0)
         b_ps0 = psum.tile([P, 512], F32, tag="A0", name="b_ps0")
         b_ps1 = psum.tile([P, 512], F32, tag="AC", name="b_ps1")
-        nc.tensor.matmul(out=b_ps0[:], lhsT=ones[:], rhs=braw[:, 0:512], start=True, stop=True)
-        nc.tensor.matmul(out=b_ps1[:, 0:256], lhsT=ones[:], rhs=braw[:, 512:768], start=True, stop=True)
-        nc.vector.tensor_copy(out=bias_bc[:, 0:512], in_=b_ps0[:])
-        nc.vector.tensor_copy(out=bias_bc[:, 512:768], in_=b_ps1[:, 0:256])
-        plain(0)
+        nc.tensor.matmul(out=b_ps0[:], lhsT=ones[:], rhs=braw[:, 0:NH], start=True, stop=True)
+        nc.tensor.matmul(out=b_ps1[:, 0:256], lhsT=ones[:], rhs=braw[:, NH:NG], start=True, stop=True)
+        vector_copy(out=bias_bc[:, 0:NH], in_=b_ps0[:])
+        vector_copy(out=bias_bc[:, NH:NG], in_=b_ps1[:, 0:256])
+        plain_products(0)
         add_bias(0)
         w_tags = ("A1", "A0", "AC", "X0", "A1", "A0")
         for a in range(2):
-            w_pe(2 * a, w_tags[2 * a])
-            w_ev(2 * a, "S")
-            w_pe(2 * a + 1, w_tags[2 * a + 1])
-            w_ev(2 * a + 1, "V")
-            w_quant(a)
-        x_pe(0, "X1")
-        x_ev(0, "S")
-        x_pe(1, "AC")
-        x_ev(1, "V")
+            w_transposes(2 * a, w_tags[2 * a])
+            w_copy(2 * a, scalar_copy)
+            w_transposes(2 * a + 1, w_tags[2 * a + 1])
+            w_copy(2 * a + 1, vector_copy)
+            w_quantise(a)
+        x_transposes(0, "X1")
+        x_copy(0, scalar_copy)
+        x_transposes(1, "AC")
+        x_copy(1, vector_copy)
         quantise(0)
-        w_pe(4, w_tags[4])
-        w_ev(4, "S")
-        w_pe(5, w_tags[5])
-        w_ev(5, "V")
-        w_quant(2)
-        hs_pe(1, "X0")
-        hs_ev(1, "S")
-        x_pe(2, "X1")
-        x_ev(2, "S")
-        x_pe(3, "X0")
-        x_ev(3, "S")
-        mx(0)
-        plain(1)
-        nc.vector.tensor_copy(out=m32[:], in_=m_bf[:])
+        w_transposes(4, w_tags[4])
+        w_copy(4, scalar_copy)
+        w_transposes(5, w_tags[5])
+        w_copy(5, vector_copy)
+        w_quantise(2)
+        hs_transposes(1, "X0")
+        hs_copy(1)
+        x_transposes(2, "X1")
+        x_copy(2, scalar_copy)
+        x_transposes(3, "X0")
+        x_copy(3, scalar_copy)
+        mx_products(0)
+        plain_products(1)
+        vector_copy(out=m32[:], in_=m_bf[:])
         quantise(1)
-        x_pe(4, "X1")
-        x_ev(4, "S")
-        x_pe(5, "X0")
-        x_ev(5, "S")
+        x_transposes(4, "X1")
+        x_copy(4, scalar_copy)
+        x_transposes(5, "X0")
+        x_copy(5, scalar_copy)
 
-        def group_at(j, off, limit):
-            if (j - off) % 2 == 0 and 0 <= (j - off) // 2 < limit:
-                return (j - off) // 2
+        def group_at(j, lag, limit):
+            if (j - lag) % 2 == 0 and 0 <= (j - lag) // 2 < limit:
+                return (j - lag) // 2
             return -1
 
-        for j in range(NPAIR + 8):
-            kk = j + LA + 2
-            do_hs = kk % 2 == 0 and 2 <= kk // 2 < NGROUP
-            if do_hs:
-                hs_pe(kk // 2, "X1")
+        for j in range(NPAIR + 3):
+            first_plain = j + PLAIN_AHEAD + 2
+            new_hs = first_plain % 2 == 0 and 2 <= first_plain // 2 < NGROUP
+            if new_hs:
+                hs_transposes(first_plain // 2, "X1")
             if j + 1 < NPAIR:
-                mx(j + 1)
+                mx_products(j + 1)
             if j < NPAIR:
                 add_mx(j)
-            if j + QL < NPAIR:
-                quantise(j + QL)
+            if j + QUANT_AHEAD < NPAIR:
+                quantise(j + QUANT_AHEAD)
             if 0 <= j - 1 < NPAIR:
                 gate_functions(j - 1)
-            if do_hs:
-                hs_ev(kk // 2, "S")
+            if new_hs:
+                hs_copy(first_plain // 2)
             g = group_at(j, 3, NG_SUM)
             if g >= 0:
                 out_tiles(g)
@@ -383,17 +381,17 @@ def tile_share_lstm_cell_t_kernel(
                 store(g, 0, 0, 4)
                 store(g, 2, 0, 4)
                 store(g, 3, 0, 4)
-            if j + XL < NPAIR:
-                if j + XL + 5 < NPAIR:
-                    load_x(j + XL + 5)
-                x_pe(2 * (j + XL), "X0")
-                x_pe(2 * (j + XL) + 1, "X1")
-                x_ev(2 * (j + XL), "S")
-                x_ev(2 * (j + XL) + 1, "S")
-            if j + LA + 1 < NPAIR:
-                plain(j + LA + 1)
-            if j + LA < NPAIR:
-                add_bias(j + LA)
+            if j + X_AHEAD < NPAIR:
+                if j + X_AHEAD + 5 < NPAIR:
+                    load_x(j + X_AHEAD + 5)
+                x_transposes(2 * (j + X_AHEAD), "X0")
+                x_transposes(2 * (j + X_AHEAD) + 1, "X1")
+                x_copy(2 * (j + X_AHEAD), scalar_copy)
+                x_copy(2 * (j + X_AHEAD) + 1, scalar_copy)
+            if j + PLAIN_AHEAD + 1 < NPAIR:
+                plain_products(j + PLAIN_AHEAD + 1)
+            if j + PLAIN_AHEAD < NPAIR:
+                add_bias(j + PLAIN_AHEAD)
             g = group_at(j, 6, NG_SUM)
             if g >= NG_OUT:
                 for tt in range(4):
@@ -401,15 +399,15 @@ def tile_share_lstm_cell_t_kernel(
                 store(g, 0, 0, 4)
                 store(g, 2, 0, 4)
                 store(g, 3, 0, 4)
-            k1 = j - 1
-            k2 = j - 2
-            if 0 <= k1 < NPAIR and k1 // 2 >= NG_SUM:
-                if k1 % 2 == 0:
-                    out_tiles(k1 // 2)
-                cell_vector(2 * k1)
-                cell_vector(2 * k1 + 1)
-            if 0 <= k2 < NPAIR and k2 // 2 >= NG_SUM:
-                outputs_vector(2 * k2)
-                outputs_vector(2 * k2 + 1)
+            k_sum = j - 1
+            k_out = j - 2
+            if 0 <= k_sum < NPAIR and k_sum // 2 >= NG_SUM:
+                if k_sum % 2 == 0:
+                    out_tiles(k_sum // 2)
+                cell_vector(2 * k_sum)
+                cell_vector(2 * k_sum + 1)
+            if 0 <= k_out < NPAIR and k_out // 2 >= NG_SUM:
+                outputs_vector(2 * k_out)
+                outputs_vector(2 * k_out + 1)
                 for which in (1, 0, 2, 3):
-                    store(k2 // 2, which, 2 * (k2 % 2), 2)
+                    store(k_out // 2, which, 2 * (k_out % 2), 2)

from contextlib import ExitStack

import concourse.mybir as mybir
from concourse.masks import make_identity

F32 = mybir.dt.float32
BF16 = mybir.dt.bfloat16
U32 = mybir.dt.uint32
U8 = mybir.dt.uint8
FP8X4 = mybir.dt.float8_e4m3fn_x4
ACT = mybir.ActivationFunctionType
ALU = mybir.AluOpType

P = 128
B = 4096
D_IN = 1024
H = 128
NG = 6 * H
NH = 4 * H
NT = B // P
NPAIR = NT // 2
NGROUP = NT // 4

X_AHEAD = 3
QUANT_AHEAD = 2
PLAIN_AHEAD = 1
NG_SUM = 7
NG_OUT = 5

FLOPS = 2 * B * (D_IN * NG + H * 512 + H * 256)
BYTES = 2 * (B * D_IN + 3 * B * H + B + NG * D_IN + 768 * H + 2 * NG) + 4 * 4 * B * H


def tile_share_lstm_cell_t_kernel(
    tc, x_in, h_minors, c_minors, s_minors, mask, weight_ih, weight_hh, weight_sh,
    bias_ih, bias_hh, bias_sh, idx, out_0, out_1, out_2, out_3,
):
    nc = tc.nc
    with ExitStack() as ctx:
        const = ctx.enter_context(tc.tile_pool(name="const", bufs=1))
        xpool = ctx.enter_context(tc.tile_pool(name="xpool", bufs=8))
        qpool = ctx.enter_context(tc.tile_pool(name="qpool", bufs=3))
        pbpool = ctx.enter_context(tc.tile_pool(name="pbpool", bufs=PLAIN_AHEAD + 1))
        gpool = ctx.enter_context(tc.tile_pool(name="gpool", bufs=5))
        opool = ctx.enter_context(tc.tile_pool(name="opool", bufs=3))
        psum = ctx.enter_context(tc.psum_pool(name="psum", bufs=1))

        xv = x_in.rearrange("(p t) k -> p t k", t=NT)
        hv = h_minors.rearrange("(p t) k -> p t k", t=NT)
        cv = c_minors.rearrange("(p t) k -> p t k", t=NT)
        sv = s_minors[idx].rearrange("(p t) k -> p t k", t=NT)
        wv = weight_ih.rearrange("(j p) k -> p j k", p=P)
        outs = [o.rearrange("(p t) k -> p t k", t=NT) for o in (out_0, out_1, out_2, out_3)]

        whh_raw = const.tile([P, 6, H], BF16)
        braw = const.tile([P, NG], BF16)
        m_bf = const.tile([P, NT], BF16)
        m32 = const.tile([P, NT], F32)
        w_raw = const.tile([P, 6, D_IN], BF16)
        h_sb = const.tile([P, NT, H], BF16)
        s_sb = const.tile([P, NT, H], BF16)
        c_sb = const.tile([P, NT, H], BF16)
        ident_f = const.tile([P, P], F32)
        ident_b = const.tile([P, P], BF16)
        ones = const.tile([P, P], BF16)
        wT = const.tile([P, NG], BF16)
        bias_bc = const.tile([P, NG], F32)
        hsT = const.tile([P, NGROUP, 2, 4, H], BF16)
        w_grp = const.tile([P, 2, NG, 2], F32, align_bytes=64)
        w_codes = const.tile([P, 2 * NG], U32, align_bytes=64)
        w_scales = const.tile([P, 2 * NG], U8, align_bytes=64)

        x_of = {}
        bank = {}
        xg_of = {}
        xq_of = {}
        pb_of = {}
        g4_of = {}
        out_of = {}

        scalar_copy = nc.scalar.copy
        vector_copy = nc.vector.tensor_copy

        def load_x(k):
            x_sb = xpool.tile([P, 2, D_IN], BF16, name="x_sb")
            nc.sync.dma_start(out=x_sb[:], in_=xv[:, 2 * k:2 * k + 2, :])
            x_of[k] = x_sb

        nc.vector.memset(braw[:], 0.0)
        nc.vector.memset(ones[:], 1.0)
        make_identity(nc, ident_b[:])
        make_identity(nc, ident_f[:])
        nc.scalar.dma_start(out=braw[0:1, :], in_=bias_ih.unsqueeze(0))
        nc.scalar.dma_start(out=braw[1:2, 0:NH], in_=bias_hh.unsqueeze(0))
        nc.scalar.dma_start(out=braw[1:2, NH:NG], in_=bias_sh.unsqueeze(0))
        nc.sync.dma_start(out=whh_raw[:, 0:4, :], in_=weight_hh.rearrange("(j p) k -> p j k", p=P))
        nc.sync.dma_start(out=whh_raw[:, 4:6, :], in_=weight_sh.rearrange("(j p) k -> p j k", p=P))
        nc.sync.dma_start(out=h_sb[:, 0:8, :], in_=hv[:, 0:8, :])
        nc.sync.dma_start(out=s_sb[:, 0:8, :], in_=sv[:, 0:8, :])
        nc.sync.dma_start(out=w_raw[:, 0:2, :], in_=wv[:, 0:2, :])
        nc.sync.dma_start(out=w_raw[:, 2:4, :], in_=wv[:, 2:4, :])
        load_x(0)
        nc.sync.dma_start(out=w_raw[:, 4:6, :], in_=wv[:, 4:6, :])
        load_x(1)
        nc.scalar.dma_start(out=m_bf[:], in_=mask.rearrange("(p t) -> p t", t=NT))
        load_x(2)
        nc.sync.dma_start(out=h_sb[:, 8:NT, :], in_=hv[:, 8:NT, :])
        nc.sync.dma_start(out=s_sb[:, 8:NT, :], in_=sv[:, 8:NT, :])
        load_x(3)
        nc.sync.dma_start(out=c_sb[:], in_=cv)
        for k in range(4, 8):
            load_x(k)

        def hs_transposes(gi, tag):
            hs_ps = psum.tile([P, 2, 4, H], BF16, tag=tag, name="hs_ps")
            bank["hs", gi] = hs_ps
            for tt in range(4):
                nc.tensor.transpose(hs_ps[:, 0, tt, :], h_sb[:, 4 * gi + tt, :], ident_b[:])
            for tt in range(4):
                nc.tensor.transpose(hs_ps[:, 1, tt, :], s_sb[:, 4 * gi + tt, :], ident_b[:])

        def hs_copy(gi):
            scalar_copy(out=hsT[:, gi], in_=bank["hs", gi][:])

        def word_transposes(rows, tag, name):
            planes = psum.tile([P, 4, P], F32, tag=tag, name=name)
            words = rows.bitcast(F32)
            for q in range(4):
                nc.tensor.transpose(planes[:, q, :], words[:, P * q:P * q + P], ident_f[:])
            return planes

        def regrouped(planes):
            return planes[:].rearrange("p (g u) r -> p g r u", g=2)

        def w_transposes(j, tag):
            bank["w", j] = word_transposes(w_raw[:, j, :], tag, "w_ps")

        def w_copy(j, copy):
            copy(out=w_grp[:, :, P * j:P * j + P, :], in_=regrouped(bank["w", j]))

        def w_quantise(a):
            for g in range(2):
                lo = g * NG + 256 * a
                nc.vector.quantize_mx(
                    out=w_codes[:, lo:lo + 256].bitcast(FP8X4), scales=w_scales[:, lo:lo + 256],
                    in_=w_grp[:, g, 256 * a:256 * a + 256, :].rearrange("p n u -> p (n u)").bitcast(BF16),
                )

        def x_transposes(t, tag):
            bank["x", t] = word_transposes(x_of[t // 2][:, t % 2, :], tag, "xt")

        def x_copy(t, copy):
            k = t // 2
            if t % 2 == 0:
                xg_new = qpool.tile([P, 2, 2, P, 2], F32, align_bytes=64, name="xg")
                xg_of[k] = xg_new
            copy(out=xg_of[k][:, t % 2], in_=regrouped(bank["x", t]))

        def quantise(k):
            xc = qpool.tile([P, 512], U32, align_bytes=64, name="xc")
            xs = qpool.tile([P, 512], U8, align_bytes=64, name="xs")
            xq_of[k] = (xc, xs)
            nc.vector.quantize_mx(
                out=xc[:].bitcast(FP8X4), scales=xs[:],
                in_=xg_of[k][:].rearrange("p t g r u -> p (t g r u)").bitcast(BF16),
            )

        def plain_products(k):
            gi = k // 2
            tt = 2 * (k % 2)
            p0 = psum.tile([P, 512], F32, tag="P0", name="p0")
            p1 = psum.tile([P, 512], F32, tag="P1", name="p1")
            pc = psum.tile([P, 512], F32, tag="PC", name="pc")
            bank["plain", k] = (p0, p1, pc)
            nc.tensor.matmul(out=p0[:], lhsT=hsT[:, gi, 0, tt, :], rhs=wT[:, 0:NH], start=True, stop=True)
            nc.tensor.matmul(out=p1[:], lhsT=hsT[:, gi, 0, tt + 1, :], rhs=wT[:, 0:NH], start=True, stop=True)
            nc.tensor.matmul(out=pc[:, 0:256], lhsT=hsT[:, gi, 1, tt, :], rhs=wT[:, NH:NG], start=True, stop=True)
            nc.tensor.matmul(out=pc[:, 256:512], lhsT=hsT[:, gi, 1, tt + 1, :], rhs=wT[:, NH:NG], start=True, stop=True)

        def add_bias(k):
            p0, p1, pc = bank["plain", k]
            pb = pbpool.tile([P, 2, NG], F32, name="pb")
            pb_of[k] = pb
            nc.vector.tensor_tensor(out=pb[:, 0, 0:NH], in0=p0[:], in1=bias_bc[:, 0:NH], op=ALU.add)
            nc.vector.tensor_tensor(out=pb[:, 1, 0:NH], in0=p1[:], in1=bias_bc[:, 0:NH], op=ALU.add)
            nc.vector.tensor_tensor(
                out=pb[:, :, NH:NG], in0=pc[:].rearrange("p (t n) -> p t n", t=2),
                in1=bias_bc[:, NH:NG].unsqueeze(1).to_broadcast([P, 2, 256]), op=ALU.add,
            )

        def mx_products(k):
            xc, xs = xq_of[k]
            a0 = psum.tile([P, 512], F32, tag="A0", name="a0")
            a1 = psum.tile([P, 512], F32, tag="A1", name="a1")
            ac = psum.tile([P, 512], F32, tag="AC", name="ac")
            bank["mx", k] = (a0, a1, ac)
            for i in range(2):
                dst = (a0, a1)[i]
                for g in range(2):
                    lo = (2 * i + g) * P
                    nc.tensor.matmul_mx(
                        out=dst[:], lhsT=xc[:, lo:lo + P].bitcast(FP8X4), lhsT_scale=xs[:, lo:lo + P],
                        rhs=w_codes[:, g * NG:g * NG + NH].bitcast(FP8X4), rhs_scale=w_scales[:, g * NG:g * NG + NH],
                        start=(g == 0), stop=(g == 1),
                    )
            for i in range(2):
                for g in range(2):
                    lo = (2 * i + g) * P
                    nc.tensor.matmul_mx(
                        out=ac[:, 256 * i:256 * i + 256], lhsT=xc[:, lo:lo + P].bitcast(FP8X4), lhsT_scale=xs[:, lo:lo + P],
                        rhs=w_codes[:, g * NG + NH:g * NG + NG].bitcast(FP8X4), rhs_scale=w_scales[:, g * NG + NH:g * NG + NG],
                        start=(g == 0), stop=(g == 1),
                    )

        def add_mx(k):
            gi = k // 2
            tt = 2 * (k % 2)
            if tt == 0:
                g4_new = gpool.tile([P, 4, NG], F32, name="g4")
                g4_of[gi] = g4_new
            g4 = g4_of[gi]
            a0, a1, ac = bank["mx", k]
            pb = pb_of[k]
            nc.vector.tensor_tensor(out=g4[:, tt, 0:NH], in0=a0[:], in1=pb[:, 0, 0:NH], op=ALU.add)
            nc.vector.tensor_tensor(out=g4[:, tt + 1, 0:NH], in0=a1[:], in1=pb[:, 1, 0:NH], op=ALU.add)
            nc.vector.tensor_tensor(
                out=g4[:, tt:tt + 2, NH:NG], in0=ac[:].rearrange("p (t n) -> p t n", t=2),
                in1=pb[:, :, NH:NG], op=ALU.add,
            )

        def gate_functions(k):
            g4 = g4_of[k // 2]
            tt = 2 * (k % 2)
            nc.scalar.activation(out=g4[:, tt:tt + 2, 0:384], in_=g4[:, tt:tt + 2, 0:384], func=ACT.Sigmoid)
            nc.scalar.activation(out=g4[:, tt:tt + 2, 384:512], in_=g4[:, tt:tt + 2, 384:512], func=ACT.Tanh)
            nc.scalar.activation(out=g4[:, tt:tt + 2, 512:768], in_=g4[:, tt:tt + 2, 512:768], func=ACT.Sigmoid)

        def out_tiles(gi):
            oh = opool.tile([P, 4, H], F32, name="oh")
            oc = opool.tile([P, 4, H], F32, name="oc")
            os_ = opool.tile([P, 2, 4, H], F32, name="os_")
            out_of[gi] = (oh, oc, os_)

        def cell_sum_gpsimd(gi):
            g4 = g4_of[gi]
            nc.gpsimd.tensor_tensor(out=g4[:, :, 128:256], in0=g4[:, :, 128:256], in1=c_sb[:, 4 * gi:4 * gi + 4, :], op=ALU.mult)
            nc.gpsimd.tensor_tensor(out=g4[:, :, 384:512], in0=g4[:, :, 0:128], in1=g4[:, :, 384:512], op=ALU.mult)
            nc.gpsimd.tensor_tensor(out=g4[:, :, 0:128], in0=g4[:, :, 128:256], in1=g4[:, :, 384:512], op=ALU.add)

        def cell_scalar(t):
            gi = t // 4
            tt = t % 4
            g4 = g4_of[gi]
            oc = out_of[gi][1]
            m = m32[:, t:t + 1]
            nc.scalar.activation(out=g4[:, tt, 128:256], in_=g4[:, tt, 0:128], func=ACT.Tanh, scale=m)
            nc.scalar.activation(out=oc[:, tt, :], in_=g4[:, tt, 0:128], func=ACT.Copy, scale=m)
            if gi < NG_OUT:
                nc.scalar.activation(out=g4[:, tt, 384:512], in_=g4[:, tt, 128:256], func=ACT.Copy, scale=m)

        def outputs_gpsimd(gi):
            g4 = g4_of[gi]
            oh, oc, os_ = out_of[gi]
            nc.gpsimd.tensor_tensor(out=oh[:], in0=g4[:, :, 256:384], in1=g4[:, :, 384:512], op=ALU.mult)
            nc.gpsimd.tensor_tensor(
                out=os_[:].rearrange("p k t c -> p t k c"),
                in0=g4[:, :, 512:768].rearrange("p t (k c) -> p t k c", k=2),
                in1=g4[:, :, 384:512].unsqueeze(2).to_broadcast([P, 4, 2, H]), op=ALU.mult,
            )

        def cell_vector(t):
            gi = t // 4
            tt = t % 4
            g4 = g4_of[gi]
            oc = out_of[gi][1]
            m = m32[:, t:t + 1]
            nc.vector.scalar_tensor_tensor(out=g4[:, tt, 128:256], in0=c_sb[:, t, :], scalar=m, in1=g4[:, tt, 128:256], op0=ALU.mult, op1=ALU.mult)
            nc.vector.scalar_tensor_tensor(out=g4[:, tt, 384:512], in0=g4[:, tt, 384:512], scalar=m, in1=g4[:, tt, 0:128], op0=ALU.mult, op1=ALU.mult)
            nc.vector.tensor_tensor(out=oc[:, tt, :], in0=g4[:, tt, 128:256], in1=g4[:, tt, 384:512], op=ALU.add)
            nc.scalar.activation(out=g4[:, tt, 128:256], in_=oc[:, tt, :], func=ACT.Tanh)

        def outputs_vector(t):
            gi = t // 4
            tt = t % 4
            g4 = g4_of[gi]
            oh, oc, os_ = out_of[gi]
            m = m32[:, t:t + 1]
            nc.vector.scalar_tensor_tensor(out=oh[:, tt, :], in0=g4[:, tt, 128:256], scalar=m, in1=g4[:, tt, 256:384], op0=ALU.mult, op1=ALU.mult)
            nc.vector.scalar_tensor_tensor(
                out=os_[:, :, tt, :], in0=g4[:, tt, 128:256].unsqueeze(1).to_broadcast([P, 2, H]), scalar=m,
                in1=g4[:, tt, 512:768].rearrange("p (k c) -> p k c", k=2), op0=ALU.mult, op1=ALU.mult,
            )

        def store(gi, which, lo, n):
            oh, oc, os_ = out_of[gi]
            src = (oh, oc, os_[:, 0], os_[:, 1])[which]
            nc.sync.dma_start(out=outs[which][:, 4 * gi + lo:4 * gi + lo + n, :], in_=src[:, lo:lo + n, :])

        wt_ps = psum.tile([P, 6, H], BF16, tag="X0", name="wt_ps")
        for j in range(6):
            nc.tensor.transpose(wt_ps[:, j, :], whh_raw[:, j, :], ident_b[:])
        scalar_copy(out=wT[:], in_=wt_ps[:].rearrange("p j k -> p (j k)"))
        hs_transposes(0, "X1")
        hs_copy(0)
        b_ps0 = psum.tile([P, 512], F32, tag="A0", name="b_ps0")
        b_ps1 = psum.tile([P, 512], F32, tag="AC", name="b_ps1")
        nc.tensor.matmul(out=b_ps0[:], lhsT=ones[:], rhs=braw[:, 0:NH], start=True, stop=True)
        nc.tensor.matmul(out=b_ps1[:, 0:256], lhsT=ones[:], rhs=braw[:, NH:NG], start=True, stop=True)
        vector_copy(out=bias_bc[:, 0:NH], in_=b_ps0[:])
        vector_copy(out=bias_bc[:, NH:NG], in_=b_ps1[:, 0:256])
        plain_products(0)
        add_bias(0)
        w_tags = ("A1", "A0", "AC", "X0", "A1", "A0")
        for a in range(2):
            w_transposes(2 * a, w_tags[2 * a])
            w_copy(2 * a, scalar_copy)
            w_transposes(2 * a + 1, w_tags[2 * a + 1])
            w_copy(2 * a + 1, vector_copy)
            w_quantise(a)
        x_transposes(0, "X1")
        x_copy(0, scalar_copy)
        x_transposes(1, "AC")
        x_copy(1, vector_copy)
        quantise(0)
        w_transposes(4, w_tags[4])
        w_copy(4, scalar_copy)
        w_transposes(5, w_tags[5])
        w_copy(5, vector_copy)
        w_quantise(2)
        hs_transposes(1, "X0")
        hs_copy(1)
        x_transposes(2, "X1")
        x_copy(2, scalar_copy)
        x_transposes(3, "X0")
        x_copy(3, scalar_copy)
        mx_products(0)
        plain_products(1)
        vector_copy(out=m32[:], in_=m_bf[:])
        quantise(1)
        x_transposes(4, "X1")
        x_copy(4, scalar_copy)
        x_transposes(5, "X0")
        x_copy(5, scalar_copy)

        def group_at(j, lag, limit):
            if (j - lag) % 2 == 0 and 0 <= (j - lag) // 2 < limit:
                return (j - lag) // 2
            return -1

        for j in range(NPAIR + 3):
            first_plain = j + PLAIN_AHEAD + 2
            new_hs = first_plain % 2 == 0 and 2 <= first_plain // 2 < NGROUP
            if new_hs:
                hs_transposes(first_plain // 2, "X1")
            if j + 1 < NPAIR:
                mx_products(j + 1)
            if j < NPAIR:
                add_mx(j)
            if j + QUANT_AHEAD < NPAIR:
                quantise(j + QUANT_AHEAD)
            if 0 <= j - 1 < NPAIR:
                gate_functions(j - 1)
            if new_hs:
                hs_copy(first_plain // 2)
            g = group_at(j, 3, NG_SUM)
            if g >= 0:
                out_tiles(g)
                cell_sum_gpsimd(g)
            g = group_at(j, 4, NG_SUM)
            if g >= 0:
                cell_scalar(4 * g)
                cell_scalar(4 * g + 1)
            g = group_at(j, 5, NG_SUM)
            if g >= 0:
                cell_scalar(4 * g + 2)
                cell_scalar(4 * g + 3)
                store(g, 1, 0, 4)
            g = group_at(j, 6, NG_OUT)
            if g >= 0:
                outputs_gpsimd(g)
                store(g, 0, 0, 4)
                store(g, 2, 0, 4)
                store(g, 3, 0, 4)
            if j + X_AHEAD < NPAIR:
                if j + X_AHEAD + 5 < NPAIR:
                    load_x(j + X_AHEAD + 5)
                x_transposes(2 * (j + X_AHEAD), "X0")
                x_transposes(2 * (j + X_AHEAD) + 1, "X1")
                x_copy(2 * (j + X_AHEAD), scalar_copy)
                x_copy(2 * (j + X_AHEAD) + 1, scalar_copy)
            if j + PLAIN_AHEAD + 1 < NPAIR:
                plain_products(j + PLAIN_AHEAD + 1)
            if j + PLAIN_AHEAD < NPAIR:
                add_bias(j + PLAIN_AHEAD)
            g = group_at(j, 6, NG_SUM)
            if g >= NG_OUT:
                for tt in range(4):
                    outputs_vector(4 * g + tt)
                store(g, 0, 0, 4)
                store(g, 2, 0, 4)
                store(g, 3, 0, 4)
            k_sum = j - 1
            k_out = j - 2
            if 0 <= k_sum < NPAIR and k_sum // 2 >= NG_SUM:
                if k_sum % 2 == 0:
                    out_tiles(k_sum // 2)
                cell_vector(2 * k_sum)
                cell_vector(2 * k_sum + 1)
            if 0 <= k_out < NPAIR and k_out // 2 >= NG_SUM:
                outputs_vector(2 * k_out)
                outputs_vector(2 * k_out + 1)
                for which in (1, 0, 2, 3):
                    store(k_out // 2, which, 2 * (k_out % 2), 2)
